import numpy as np
import ml_dtypes


def mxq(x, axis, fmt="e4m3"):
    dtype, down = {"e4m3": (ml_dtypes.float8_e4m3fn, 7), "e5m2": (ml_dtypes.float8_e5m2, 14)}[fmt]
    v = np.moveaxis(np.asarray(x, np.float32).astype(ml_dtypes.bfloat16).astype(np.float64), axis, -1)
    blocks = v.reshape(v.shape[:-1] + (-1, 32))
    amax = np.abs(blocks).max(-1, keepdims=True)
    byte = np.maximum(np.where(amax > 0, np.frexp(amax)[1] - 1 + 127, 0) - down, 1)
    scale = np.exp2(byte - 127.0)
    codes = (blocks / scale).astype(np.float32).astype(dtype).astype(np.float64)
    return np.moveaxis((codes * scale).reshape(v.shape), -1, axis)


WIDE = False


def mx_kscale(k):
    if not WIDE:
        return np.ones(k)
    levels = np.array([10, -10, 5, -5, 0])
    a = np.random.permutation(np.resize(levels, k // 512 * 4)).reshape(k // 512, 4)
    idx = np.arange(k)
    return np.exp2(a[idx // 512, idx % 128 // 32])


BF16 = ml_dtypes.bfloat16


def bf(x):
    return np.asarray(x, np.float32).astype(BF16)


def f64(x):
    return np.asarray(x).astype(np.float64)


E2M1 = np.array([0.0, 0.5, 1.0, 1.5, 2.0, 3.0, 4.0, 6.0, -0.0, -0.5, -1.0, -1.5, -2.0, -3.0, -4.0, -6.0])


def pack_weight(w, fmt):
    k, n = w.shape
    w = f64(bf(w)).reshape(k // 32, 32, n)
    amax = np.abs(w).max(1)
    if fmt == "e4m3":
        byte = np.frexp(amax)[1] - 1 + 127 - 7
    else:
        mant, ex = np.frexp(amax / 6.0)
        byte = np.where(mant > 0.5, ex, ex - 1) + 127
    byte = np.clip(np.where(amax > 0, byte, 1), 1, 254)
    scaled = (w * np.exp2(127.0 - byte)[:, None, :]).reshape(k, n).astype(np.float32)
    by_word = np.ascontiguousarray(scaled.reshape(k // 512, 128, 4, n).transpose(0, 1, 3, 2))
    if fmt == "e4m3":
        words = by_word.astype(ml_dtypes.float8_e4m3fn).view(np.uint8)
    else:
        c = by_word.astype(ml_dtypes.float4_e2m1fn).view(np.uint8) & 0xF
        words = c[..., 0::2] | (c[..., 1::2] << 4)
    return np.ascontiguousarray(words), np.ascontiguousarray(byte.astype(np.uint8).reshape(k // 512, 16, n))


def unpack_weight(words, scales, fmt):
    g, p, n, _ = words.shape
    if fmt == "e4m3":
        vals = np.ascontiguousarray(words).view(ml_dtypes.float8_e4m3fn).astype(np.float64)
    else:
        nib = np.empty((g, p, n, 4), np.uint8)
        nib[..., 0::2] = words & 0xF
        nib[..., 1::2] = words >> 4
        vals = E2M1[nib]
    vals = vals * np.repeat(np.exp2(scales.astype(np.float64) - 127.0), 8, axis=1)[..., None]
    return vals.transpose(0, 1, 3, 2).reshape(g * 512, n)


B, PED, NED, CED = 128, 1280, 512, 2048
Q = PED // 4
FEAT = 2 * PED + 3 * NED


def leaky(v):
    return np.where(v >= 0.0, v, 0.01 * v)


def point_enc(xy, wsx, bsx, wcx, bcx, wsy, bsy, wcy, bcy):
    x = xy[:, 0:1]
    y = xy[:, 1:2]
    return np.concatenate([np.sin(x * wsx + bsx), np.cos(x * wcx + bcx), np.sin(y * wsy + bsy), np.cos(y * wcy + bcy)], axis=-1)


def num_enc(t, w, b):
    return leaky(t[:, None] * w + b)


def setup_inputs():
    s = np.array(mx_kscale(FEAT), dtype=np.float64)
    s[:2 * PED] = 1.0
    t = mx_kscale(CED)
    d = {'src_xy': bf(np.random.standard_normal((B, 2))), 'dst_xy': bf(np.random.standard_normal((B, 2))),
         'time_s': bf(np.random.uniform(size=B)), 'wait_src': bf(np.random.uniform(size=B)), 'wait_dst': bf(np.random.uniform(size=B))}
    for pfx in ('src', 'dst'):
        for part in ('wsx', 'bsx', 'wcx', 'bcx', 'wsy', 'bsy', 'wcy', 'bcy'):
            d[pfx + '_' + part] = bf(np.random.standard_normal(Q) * (1.0 if part[0] == 'w' else 0.1))
    for i, pfx in enumerate(('t', 'ws', 'wd')):
        sn = s[2 * PED + i * NED:2 * PED + (i + 1) * NED]
        d[pfx + '_w'] = bf(np.random.standard_normal(NED) * sn)
        d[pfx + '_b'] = bf(np.random.standard_normal(NED) * 0.1 * sn)
    d['W1_words'], d['W1_scales'] = pack_weight(np.random.standard_normal((FEAT, CED)) * 1.5 / np.sqrt(FEAT) / s[:, None] * t[None, :], 'e4m3')
    d['b1'] = bf(np.random.standard_normal(CED) * 0.1 * t)
    d['W2_words'], d['W2_scales'] = pack_weight(np.random.standard_normal((CED, CED)) * 1.5 / np.sqrt(CED) / t[:, None], 'e4m3')
    d['b2'] = bf(np.random.standard_normal(CED) * 0.1)
    return d


def reference(src_xy, dst_xy, time_s, wait_src, wait_dst,
              src_wsx, src_bsx, src_wcx, src_bcx, src_wsy, src_bsy, src_wcy, src_bcy,
              dst_wsx, dst_bsx, dst_wcx, dst_bcx, dst_wsy, dst_bsy, dst_wcy, dst_bcy,
              t_w, t_b, ws_w, ws_b, wd_w, wd_b,
              W1_words, W1_scales, b1, W2_words, W2_scales, b2):
    feats = np.concatenate([
        point_enc(f64(src_xy), f64(src_wsx), f64(src_bsx), f64(src_wcx), f64(src_bcx),
                        f64(src_wsy), f64(src_bsy), f64(src_wcy), f64(src_bcy)),
        point_enc(f64(dst_xy), f64(dst_wsx), f64(dst_bsx), f64(dst_wcx), f64(dst_bcx),
                        f64(dst_wsy), f64(dst_bsy), f64(dst_wcy), f64(dst_bcy)),
        num_enc(f64(time_s), f64(t_w), f64(t_b)),
        num_enc(f64(wait_src), f64(ws_w), f64(ws_b)),
        num_enc(f64(wait_dst), f64(wd_w), f64(wd_b)),
    ], axis=-1)
    h = leaky((mxq(feats, 1, 'e4m3') @ unpack_weight(W1_words, W1_scales, 'e4m3')) + f64(b1))
    return leaky((mxq(h, 1, 'e4m3') @ unpack_weight(W2_words, W2_scales, 'e4m3')) + f64(b2))

@@ -1,0 +1,362 @@
+import math
+from contextlib import ExitStack
+
+import concourse.bass as bass
+import concourse.mybir as mybir
+import concourse.tile as tile
+from concourse.masks import make_identity
+
+F32 = mybir.dt.float32
+BF16 = mybir.dt.bfloat16
+I32 = mybir.dt.int32
+U32 = mybir.dt.uint32
+U8 = mybir.dt.uint8
+FP8X4 = mybir.dt.float8_e4m3fn_x4
+ALU = mybir.AluOpType
+ACTF = mybir.ActivationFunctionType
+
+P = 128
+FEAT = 4096
+HID = 2048
+G1 = 8
+G2 = 4
+NT = 512
+TRIG_G = 5
+SEG = 320
+FLOPS = 2 * 128 * (FEAT * HID + HID * HID)
+TWO_PI = 2.0 * math.pi
+INV_TWO_PI = 1.0 / TWO_PI
+
+
+def row(vec):
+    return vec.rearrange("(o n) -> o n", o=1)
+
+
+def tile_claimencoder_w_kernel(
+    tc,
+    src_xy, dst_xy, time_s, wait_src, wait_dst,
+    src_wsx, src_bsx, src_wcx, src_bcx, src_wsy, src_bsy, src_wcy, src_bcy,
+    dst_wsx, dst_bsx, dst_wcx, dst_bcx, dst_wsy, dst_bsy, dst_wcy, dst_bcy,
+    t_w, t_b, ws_w, ws_b, wd_w, wd_b,
+    W1_words, W1_scales, b1, W2_words, W2_scales, b2,
+    out,
+):
+    nc = tc.nc
+    with ExitStack() as ctx:
+        ctx.enter_context(tc.manual_schedule())
+        keep = ctx.enter_context(tc.tile_pool(name="keep", bufs=1))
+        rot = ctx.enter_context(tc.tile_pool(name="rot", bufs=2))
+        outp = ctx.enter_context(tc.tile_pool(name="outp", bufs=4))
+        ps = ctx.enter_context(tc.psum_pool(name="ps", bufs=1))
+
+        def bank(i, shape, dtype, name):
+            return ps.tile(shape, dtype, tag="b%d" % i, name=name)
+
+        par = keep.tile([P, FEAT], BF16, name="par")
+        inp = keep.tile([P, 544], BF16, name="inp")
+        brow = keep.tile([P, 2 * HID], BF16, name="brow")
+        cosi = keep.tile([P, 640], BF16, name="cosi")
+        warm = keep.tile([P, 2], F32, name="warm")
+        ident = keep.tile([P, P], BF16, name="ident")
+        planes = keep.tile([P, 3, HID], U8, name="planes", align_bytes=64)
+        w1 = keep.tile([P, G1, HID], I32, name="w1", align_bytes=64)
+        w2 = keep.tile([P, G2, HID], I32, name="w2", align_bytes=64)
+        phase = keep.tile([P, TRIG_G], F32, name="phase")
+        sbias = keep.tile([P, TRIG_G], F32, name="sbias")
+        fgrp = keep.tile([P, G1, P, 4], BF16, name="fgrp", align_bytes=64)
+        fcod = keep.tile([P, G1, P], U32, name="fcod", align_bytes=64)
+        fscl = keep.tile([P, G1, P], U8, name="fscl", align_bytes=64)
+        bbc = keep.tile([P, 2, HID], BF16, name="bbc")
+        hb = keep.tile([P, HID], BF16, name="hb")
+        hgrp = keep.tile([P, G2, P, 4], BF16, name="hgrp", align_bytes=64)
+        hcod = keep.tile([P, G2, P], U32, name="hcod", align_bytes=64)
+        hscl = keep.tile([P, G2, P], U8, name="hscl", align_bytes=64)
+
+        nc.vector.memset(par[:, 0:1280].bitcast(I32), 0)
+        nc.vector.memset(inp[:].bitcast(I32), 0)
+        nc.vector.memset(inp[0:1, 0:384], 1.0)
+        nc.vector.memset(inp[0:1, 384:416], 0.25)
+        nc.vector.memset(inp[0:1, 416:544], 1.0)
+        nc.vector.memset(warm[:], 0.0)
+        nc.vector.memset(par[:, 1280:2560].bitcast(I32), 0)
+        nc.vector.memset(cosi[:].bitcast(I32), 0)
+        nc.vector.memset(
+            cosi[0:1, :].rearrange("o (s h c) -> o s h c", h=2, c=80)[:, :, 1, :], 1.0
+        )
+        nc.vector.memset(par[:, 2560:4096].bitcast(I32), 0)
+        nc.vector.memset(planes[:].rearrange("p a n -> p (a n)").bitcast(I32), 0)
+        nc.vector.memset(brow[:].bitcast(I32), 0)
+
+        make_identity(nc, ident[:])
+        nc.scalar.activation(out=warm[:, 1:2], in_=warm[:, 0:1], func=ACTF.Sin)
+
+        def small(eng, dst, vec):
+            eng.dma_start(out=dst, in_=vec)
+
+        def xy_rows(eng, r, xy, which):
+            flat = xy.rearrange("(o c) t -> o (c t)", o=1)
+            if which == 0:
+                small(eng, inp[r:r + 1, 0:256], flat)
+            else:
+                small(eng, inp[r:r + 1, 0:255], flat[:, 1:256])
+
+        def seg(eng, r, s, wv, bv):
+            small(eng, par[r:r + 1, SEG * s:SEG * (s + 1)], row(wv))
+            small(eng, par[0:1, SEG * s:SEG * (s + 1)], row(bv))
+
+        def scale_tile(a, scales, g0, q):
+            nc.sync.dma_start(
+                out=planes[32 * q:32 * q + 16, a, :].bitcast(I32),
+                in_=scales[g0:g0 + 4, 4 * q:4 * q + 4, :].bitcast(I32),
+            )
+
+        def w1_pair(g, h):
+            nc.sync.dma_start(
+                out=w1[:, g:g + 2, 1024 * h:1024 * (h + 1)],
+                in_=W1_words[g:g + 2].rearrange("g p n t -> p g (n t)")[
+                    :, :, 4096 * h:4096 * (h + 1)
+                ].bitcast(I32),
+            )
+
+        sy = nc.sync
+        xy_rows(sy, 1, src_xy, 0)
+        xy_rows(sy, 2, src_xy, 1)
+        xy_rows(sy, 3, dst_xy, 0)
+        xy_rows(sy, 4, dst_xy, 1)
+        seg(sy, 1, 0, src_wsx, src_bsx)
+        seg(sy, 1, 1, src_wcx, src_bcx)
+        seg(sy, 2, 2, src_wsy, src_bsy)
+        seg(sy, 2, 3, src_wcy, src_bcy)
+        seg(sy, 3, 4, dst_wsx, dst_bsx)
+        w1_pair(0, 0)
+        w1_pair(2, 0)
+        for q in range(4):
+            scale_tile(0, W1_scales, 0, q)
+        seg(sy, 3, 5, dst_wcx, dst_bcx)
+        w1_pair(4, 0)
+        w1_pair(6, 0)
+        seg(sy, 4, 6, dst_wsy, dst_bsy)
+        seg(sy, 4, 7, dst_wcy, dst_bcy)
+        small(sy, brow[0:1, 0:HID], row(b1))
+        small(sy, brow[0:1, HID:2 * HID], row(b2))
+        w1_pair(0, 1)
+        w1_pair(2, 1)
+        for q in range(4):
+            scale_tile(1, W1_scales, 4, q)
+        w1_pair(4, 1)
+        w1_pair(6, 1)
+        for q in range(4):
+            scale_tile(2, W2_scales, 0, q)
+        for g in range(2):
+            nc.sync.dma_start(
+                out=w2[:, g, :],
+                in_=W2_words[g].rearrange("p n t -> p (n t)").bitcast(I32),
+            )
+        for j in range(4):
+            nc.sync.dma_start(
+                out=w2[:, 2:4, NT * j:NT * (j + 1)],
+                in_=W2_words[2:4].rearrange("g p n t -> p g (n t)")[
+                    :, :, 4 * NT * j:4 * NT * (j + 1)
+                ].bitcast(I32),
+            )
+
+        gp = nc.gpsimd
+        nums = ((time_s, t_w, t_b), (wait_src, ws_w, ws_b), (wait_dst, wd_w, wd_b))
+        for i, (sv, wv, bv) in enumerate(nums):
+            small(gp, inp[5 + i:6 + i, 256:384], row(sv))
+        for i, (sv, wv, bv) in enumerate(nums):
+            c0 = 2560 + 512 * i
+            small(gp, par[5 + i:6 + i, c0:c0 + 512], row(wv))
+            small(gp, par[0:1, c0:c0 + 512], row(bv))
+
+        ph_ps = bank(6, [P, 16, 32], F32, "ph_ps")
+        for g in range(TRIG_G):
+            nc.tensor.matmul(
+                out=ph_ps[:, g, :], lhsT=cosi[:, P * g:P * (g + 1)], rhs=inp[:, 384:416],
+                start=True, stop=True,
+            )
+        nc.vector.tensor_copy(out=phase[:], in_=ph_ps[:, 0:TRIG_G, 0])
+        nc.vector.tensor_scalar(
+            out=sbias[:], in0=ph_ps[:, 0:TRIG_G, 0], scalar1=TWO_PI, scalar2=None, op0=ALU.mult
+        )
+
+        zbank = {0: 2, 1: 3, 2: 4, 3: 5, 4: 2, 5: 3, 6: 4, 7: 5}
+        ztile = {}
+
+        def z_block(g):
+            zb = bank(zbank[g], [P, 4, P], F32, "z%d" % g)
+            ztile[g] = zb
+            rhs = inp[:, 0:256:2] if g < TRIG_G else inp[:, 256:384]
+            for t in range(4):
+                nc.tensor.matmul(
+                    out=zb[:, t, :], lhsT=par[:, 512 * g + t:512 * (g + 1):4], rhs=rhs,
+                    start=True, stop=True,
+                )
+
+        def trig(g):
+            zf = ztile[g][:].rearrange("p t c -> p (t c)")
+            turns = rot.tile([P, NT], I32, tag="turns", name="turns")
+            frac = rot.tile([P, NT], F32, tag="frac", name="frac")
+            nc.vector.tensor_scalar(
+                out=turns[:], in0=zf, scalar1=INV_TWO_PI, scalar2=phase[:, g:g + 1],
+                op0=ALU.mult, op1=ALU.add,
+            )
+            nc.vector.scalar_tensor_tensor(
+                out=frac[:], in0=zf, scalar=INV_TWO_PI, in1=turns[:],
+                op0=ALU.mult, op1=ALU.subtract,
+            )
+            nc.scalar.activation(
+                out=fgrp[:, g], in_=frac[:].rearrange("p (t c) -> p c t", t=4),
+                func=ACTF.Sin, bias=sbias[:, g:g + 1], scale=TWO_PI,
+            )
+
+        def num(g):
+            zb = ztile[g]
+            small_v = rot.tile([P, 4, P], F32, tag="leak", name="leak")
+            nc.scalar.activation(out=small_v[:], in_=zb[:], func=ACTF.Copy, scale=0.01)
+            nc.vector.tensor_tensor(
+                out=fgrp[:, g], in0=zb[:].rearrange("p t c -> p c t"),
+                in1=small_v[:].rearrange("p t c -> p c t"), op=ALU.max,
+            )
+
+        def quant_f(g):
+            nc.vector.quantize_mx(
+                out=fcod[:, g, :].bitcast(FP8X4), scales=fscl[:, g, :],
+                in_=fgrp[:, g].rearrange("p c t -> p (c t)"),
+            )
+
+        acc1 = {}
+
+        def l1(g, tiles, first, last):
+            k = 4 * (g % 4)
+            for j in tiles:
+                nc.tensor.matmul_mx(
+                    out=acc1[j][:],
+                    lhsT=fcod[:, g, :].bitcast(FP8X4), lhsT_scale=fscl[:, g, :],
+                    rhs=w1[:, g, NT * j:NT * (j + 1)].bitcast(FP8X4),
+                    rhs_scale=planes[k:P, g // 4, NT * j:NT * (j + 1)],
+                    start=first, stop=last,
+                )
+
+        def bias_bc(layer, i, b):
+            bb = bank(b, [P, NT], F32, "bb%d_%d" % (layer, i))
+            c0 = HID * layer + NT * i
+            nc.tensor.matmul(
+                out=bb[:], lhsT=inp[:, 416:544], rhs=brow[:, c0:c0 + NT], start=True, stop=True
+            )
+            nc.scalar.copy(out=bbc[:, layer, NT * i:NT * (i + 1)], in_=bb[:])
+
+        def h_epilogue(j):
+            pre = rot.tile([P, NT], F32, tag="pre", name="pre")
+            nc.vector.tensor_tensor(
+                out=pre[:], in0=acc1[j][:], in1=bbc[:, 0, NT * j:NT * (j + 1)], op=ALU.add
+            )
+            nc.vector.scalar_tensor_tensor(
+                out=hb[:, NT * j:NT * (j + 1)], in0=pre[:], scalar=0.01, in1=pre[:],
+                op0=ALU.mult, op1=ALU.max,
+            )
+
+        def h_transpose(j, b):
+            xt = bank(b, [P, 8, P], BF16, "xt%d" % j)
+            for t in range(4):
+                nc.tensor.transpose(
+                    out=xt[:, t, :], in_=hb[:, NT * j + t:NT * (j + 1):4], identity=ident[:]
+                )
+            nc.scalar.copy(out=hgrp[:, j], in_=xt[:, 0:4, :].rearrange("p t c -> p c t"))
+
+        def quant_h(j):
+            nc.vector.quantize_mx(
+                out=hcod[:, j, :].bitcast(FP8X4), scales=hscl[:, j, :],
+                in_=hgrp[:, j].rearrange("p c t -> p (c t)"),
+            )
+
+        z_block(0)
+        z_block(1)
+        z_block(2)
+        z_block(3)
+        trig(0)
+        trig(1)
+        quant_f(0)
+        z_block(4)
+        acc1[0] = bank(0, [P, NT], F32, "acc1_0")
+        acc1[1] = bank(1, [P, NT], F32, "acc1_1")
+        l1(0, (0, 1), True, False)
+        trig(2)
+        quant_f(1)
+        z_block(5)
+        l1(1, (0, 1), False, False)
+        trig(3)
+        quant_f(2)
+        z_block(6)
+        l1(2, (0, 1), False, False)
+        trig(4)
+        quant_f(3)
+        z_block(7)
+        l1(3, (0, 1), False, False)
+        num(5)
+        quant_f(4)
+        l1(4, (0, 1), False, False)
+        num(6)
+        quant_f(5)
+        num(7)
+        quant_f(6)
+        quant_f(7)
+        for i in range(4):
+            bias_bc(0, i, 6 + i % 2)
+        l1(5, (0, 1), False, False)
+        l1(6, (0, 1), False, False)
+        l1(7, (0, 1), False, True)
+
+        acc1[2] = bank(2, [P, NT], F32, "acc1_2")
+        acc1[3] = bank(3, [P, NT], F32, "acc1_3")
+        h_epilogue(0)
+        h_epilogue(1)
+        l1(0, (2, 3), True, False)
+        l1(1, (2, 3), False, False)
+        h_transpose(0, 6)
+        l1(2, (2, 3), False, False)
+        l1(3, (2, 3), False, False)
+        h_transpose(1, 7)
+        quant_h(0)
+        quant_h(1)
+        l1(4, (2, 3), False, False)
+        l1(5, (2, 3), False, False)
+        for i in range(4):
+            bias_bc(1, i, 6 + i % 2)
+        l1(6, (2, 3), False, False)
+        l1(7, (2, 3), False, True)
+        h_epilogue(2)
+        h_epilogue(3)
+        h_transpose(2, 6)
+        h_transpose(3, 7)
+        quant_h(2)
+        quant_h(3)
+
+        acc2bank = (4, 5, 0, 1)
+        acc2 = [bank(acc2bank[j], [P, NT], F32, "acc2_%d" % j) for j in range(4)]
+
+        def l2(g, j, first, last):
+            k = 4 * g
+            nc.tensor.matmul_mx(
+                out=acc2[j][:],
+                lhsT=hcod[:, g, :].bitcast(FP8X4), lhsT_scale=hscl[:, g, :],
+                rhs=w2[:, g, NT * j:NT * (j + 1)].bitcast(FP8X4),
+                rhs_scale=planes[k:P, 2, NT * j:NT * (j + 1)],
+                start=first, stop=last,
+            )
+
+        for g in range(2):
+            for j in range(4):
+                l2(g, j, g == 0, False)
+        for j in range(4):
+            l2(2, j, False, False)
+            l2(3, j, False, True)
+            pre = rot.tile([P, NT], F32, tag="pre", name="pre")
+            res = outp.tile([P, NT], F32, tag="res", name="res")
+            nc.vector.tensor_tensor(
+                out=pre[:], in0=acc2[j][:], in1=bbc[:, 1, NT * j:NT * (j + 1)], op=ALU.add
+            )
+            nc.vector.scalar_tensor_tensor(
+                out=res[:], in0=pre[:], scalar=0.01, in1=pre[:], op0=ALU.mult, op1=ALU.max
+            )
+            nc.sync.dma_start(out=out[:, NT * j:NT * (j + 1)], in_=res[:])

@@ -53,8 +53,10 @@ def tile_claimencoder_w_kernel(
             return ps.tile(shape, dtype, tag="b%d" % i, name=name)
 
         par = keep.tile([P, FEAT], BF16, name="par")
-        inp = keep.tile([P, 544], BF16, name="inp")
-        brow = keep.tile([P, 2 * HID], BF16, name="brow")
+        inp_s = keep.tile([P, 256], BF16, name="inp_s")
+        inp_d = keep.tile([P, 256], BF16, name="inp_d")
+        inp_n = keep.tile([P, P], BF16, name="inp_n")
+        cst = keep.tile([P, 160], BF16, name="cst")
         cosi = keep.tile([P, 640], BF16, name="cosi")
         warm = keep.tile([P, 2], F32, name="warm")
         ident = keep.tile([P, P], BF16, name="ident")
@@ -72,42 +74,54 @@ def tile_claimencoder_w_kernel(
         hcod = keep.tile([P, G2, P], U32, name="hcod", align_bytes=64)
         hscl = keep.tile([P, G2, P], U8, name="hscl", align_bytes=64)
 
-        nc.vector.memset(par[:, 0:1280].bitcast(I32), 0)
-        nc.vector.memset(inp[:].bitcast(I32), 0)
-        nc.vector.memset(inp[0:1, 0:384], 1.0)
-        nc.vector.memset(inp[0:1, 384:416], 0.25)
-        nc.vector.memset(inp[0:1, 416:544], 1.0)
-        nc.vector.memset(warm[:], 0.0)
-        nc.vector.memset(par[:, 1280:2560].bitcast(I32), 0)
-        nc.vector.memset(cosi[:].bitcast(I32), 0)
+        def zero(ap):
+            nc.vector.memset(ap.bitcast(I32), 0)
+
+        zero(inp_s[:])
+        nc.vector.memset(inp_s[0:1, :], 1.0)
+        zero(par[:, 0:2048])
+        zero(inp_d[:])
+        nc.vector.memset(inp_d[32:33, :], 1.0)
+        zero(par[:, 2048:4096])
+        zero(cst[:])
+        nc.vector.memset(cst[0:1, 0:32], 0.25)
+        nc.vector.memset(cst[64:65, 32:160], 1.0)
+        zero(cosi[:])
         nc.vector.memset(
             cosi[0:1, :].rearrange("o (s h c) -> o s h c", h=2, c=80)[:, :, 1, :], 1.0
         )
-        nc.vector.memset(par[:, 2560:4096].bitcast(I32), 0)
-        nc.vector.memset(planes[:].rearrange("p a n -> p (a n)").bitcast(I32), 0)
-        nc.vector.memset(brow[:].bitcast(I32), 0)
+        zero(inp_n[:])
+        nc.vector.memset(inp_n[0:1, :], 1.0)
+        nc.vector.memset(warm[:], 0.0)
+        zero(planes[:].rearrange("p a n -> p (a n)"))
 
         make_identity(nc, ident[:])
         nc.scalar.activation(out=warm[:, 1:2], in_=warm[:, 0:1], func=ACTF.Sin)
 
-        def small(eng, dst, vec):
-            eng.dma_start(out=dst, in_=vec)
-
-        def xy_rows(eng, r, xy, which):
+        def xy_row(eng, dst, r, xy, which):
             flat = xy.rearrange("(o c) t -> o (c t)", o=1)
             if which == 0:
-                small(eng, inp[r:r + 1, 0:256], flat)
+                eng.dma_start(out=dst[r:r + 1, 0:256], in_=flat)
             else:
-                small(eng, inp[r:r + 1, 0:255], flat[:, 1:256])
+                eng.dma_start(out=dst[r:r + 1, 0:255], in_=flat[:, 1:256])
 
-        def seg(eng, r, s, wv, bv):
-            small(eng, par[r:r + 1, SEG * s:SEG * (s + 1)], row(wv))
-            small(eng, par[0:1, SEG * s:SEG * (s + 1)], row(bv))
+        def seg_w(eng, r, s, wv):
+            eng.dma_start(out=par[r:r + 1, SEG * s:SEG * (s + 1)], in_=row(wv))
 
-        def scale_tile(a, scales, g0, q):
+        def seg_b(eng, s, bv):
+            r = 0 if s < 4 else 32
+            eng.dma_start(out=par[r:r + 1, SEG * s:SEG * (s + 1)], in_=row(bv))
+
+        def scale_tile(a, scales, g0):
+            for q in range(4):
+                nc.sync.dma_start(
+                    out=planes[32 * q:32 * q + 16, a, :].bitcast(I32),
+                    in_=scales[g0:g0 + 4, 4 * q:4 * q + 4, :].bitcast(I32),
+                )
+
+        def w1_full(g):
             nc.sync.dma_start(
-                out=planes[32 * q:32 * q + 16, a, :].bitcast(I32),
-                in_=scales[g0:g0 + 4, 4 * q:4 * q + 4, :].bitcast(I32),
+                out=w1[:, g, :], in_=W1_words[g].rearrange("p n t -> p (n t)").bitcast(I32)
             )
 
         def w1_pair(g, h):
@@ -119,34 +133,33 @@ def tile_claimencoder_w_kernel(
             )
 
         sy = nc.sync
-        xy_rows(sy, 1, src_xy, 0)
-        xy_rows(sy, 2, src_xy, 1)
-        xy_rows(sy, 3, dst_xy, 0)
-        xy_rows(sy, 4, dst_xy, 1)
-        seg(sy, 1, 0, src_wsx, src_bsx)
-        seg(sy, 1, 1, src_wcx, src_bcx)
-        seg(sy, 2, 2, src_wsy, src_bsy)
-        seg(sy, 2, 3, src_wcy, src_bcy)
-        seg(sy, 3, 4, dst_wsx, dst_bsx)
-        w1_pair(0, 0)
-        w1_pair(2, 0)
-        for q in range(4):
-            scale_tile(0, W1_scales, 0, q)
-        seg(sy, 3, 5, dst_wcx, dst_bcx)
-        w1_pair(4, 0)
+        xy_row(sy, inp_s, 1, src_xy, 0)
+        xy_row(sy, inp_s, 2, src_xy, 1)
+        seg_w(sy, 1, 0, src_wsx)
+        seg_b(sy, 0, src_bsx)
+        seg_w(sy, 1, 1, src_wcx)
+        seg_b(sy, 1, src_bcx)
+        sy.dma_start(out=par[64:65, 0:HID], in_=row(b1))
+        seg_w(sy, 2, 2, src_wsy)
+        seg_b(sy, 2, src_bsy)
+        seg_w(sy, 2, 3, src_wcy)
+        seg_b(sy, 3, src_bcy)
+        xy_row(sy, inp_d, 3, dst_xy, 0)
+        xy_row(sy, inp_d, 4, dst_xy, 1)
+        seg_w(sy, 3, 4, dst_wsx)
+        seg_b(sy, 4, dst_bsx)
+        w1_full(0)
+        w1_full(1)
+        scale_tile(0, W1_scales, 0)
+        w1_full(2)
+        sy.dma_start(out=par[64:65, HID:2 * HID], in_=row(b2))
+        w1_full(3)
+        w1_full(4)
+        scale_tile(1, W1_scales, 4)
+        w1_full(5)
         w1_pair(6, 0)
-        seg(sy, 4, 6, dst_wsy, dst_bsy)
-        seg(sy, 4, 7, dst_wcy, dst_bcy)
-        small(sy, brow[0:1, 0:HID], row(b1))
-        small(sy, brow[0:1, HID:2 * HID], row(b2))
-        w1_pair(0, 1)
-        w1_pair(2, 1)
-        for q in range(4):
-            scale_tile(1, W1_scales, 4, q)
-        w1_pair(4, 1)
         w1_pair(6, 1)
-        for q in range(4):
-            scale_tile(2, W2_scales, 0, q)
+        scale_tile(2, W2_scales, 0)
         for g in range(2):
             nc.sync.dma_start(
                 out=w2[:, g, :],
@@ -161,18 +174,24 @@ def tile_claimencoder_w_kernel(
             )
 
         gp = nc.gpsimd
+        seg_w(gp, 3, 5, dst_wcx)
+        seg_b(gp, 5, dst_bcx)
+        seg_w(gp, 4, 6, dst_wsy)
+        seg_b(gp, 6, dst_bsy)
+        seg_w(gp, 4, 7, dst_wcy)
+        seg_b(gp, 7, dst_bcy)
         nums = ((time_s, t_w, t_b), (wait_src, ws_w, ws_b), (wait_dst, wd_w, wd_b))
         for i, (sv, wv, bv) in enumerate(nums):
-            small(gp, inp[5 + i:6 + i, 256:384], row(sv))
+            gp.dma_start(out=inp_n[5 + i:6 + i, :], in_=row(sv))
         for i, (sv, wv, bv) in enumerate(nums):
             c0 = 2560 + 512 * i
-            small(gp, par[5 + i:6 + i, c0:c0 + 512], row(wv))
-            small(gp, par[0:1, c0:c0 + 512], row(bv))
+            gp.dma_start(out=par[5 + i:6 + i, c0:c0 + 512], in_=row(wv))
+            gp.dma_start(out=par[0:1, c0:c0 + 512], in_=row(bv))
 
-        ph_ps = bank(6, [P, 16, 32], F32, "ph_ps")
+        ph_ps = bank(7, [P, 16, 32], F32, "ph_ps")
         for g in range(TRIG_G):
             nc.tensor.matmul(
-                out=ph_ps[:, g, :], lhsT=cosi[:, P * g:P * (g + 1)], rhs=inp[:, 384:416],
+                out=ph_ps[:, g, :], lhsT=cosi[:, P * g:P * (g + 1)], rhs=cst[:, 0:32],
                 start=True, stop=True,
             )
         nc.vector.tensor_copy(out=phase[:], in_=ph_ps[:, 0:TRIG_G, 0])
@@ -180,23 +199,30 @@ def tile_claimencoder_w_kernel(
             out=sbias[:], in0=ph_ps[:, 0:TRIG_G, 0], scalar1=TWO_PI, scalar2=None, op0=ALU.mult
         )
 
-        zbank = {0: 2, 1: 3, 2: 4, 3: 5, 4: 2, 5: 3, 6: 4, 7: 5}
+        zbank = {0: 4, 1: 5, 2: 6, 3: 4, 4: 5, 5: 6, 6: 4, 7: 5}
+        zrhs = {0: (inp_s,), 1: (inp_s,), 2: (inp_s, inp_d), 3: (inp_d,), 4: (inp_d,)}
         ztile = {}
+        frac_of = {}
 
         def z_block(g):
             zb = bank(zbank[g], [P, 4, P], F32, "z%d" % g)
             ztile[g] = zb
-            rhs = inp[:, 0:256:2] if g < TRIG_G else inp[:, 256:384]
+            if g < TRIG_G:
+                rhs = [src[:, 0:256:2] for src in zrhs[g]]
+            else:
+                rhs = [inp_n[:]]
             for t in range(4):
-                nc.tensor.matmul(
-                    out=zb[:, t, :], lhsT=par[:, 512 * g + t:512 * (g + 1):4], rhs=rhs,
-                    start=True, stop=True,
-                )
+                for i, r in enumerate(rhs):
+                    nc.tensor.matmul(
+                        out=zb[:, t, :], lhsT=par[:, 512 * g + t:512 * (g + 1):4], rhs=r,
+                        start=(i == 0), stop=(i == len(rhs) - 1),
+                    )
 
-        def trig(g):
+        def trig_v(g):
             zf = ztile[g][:].rearrange("p t c -> p (t c)")
             turns = rot.tile([P, NT], I32, tag="turns", name="turns")
             frac = rot.tile([P, NT], F32, tag="frac", name="frac")
+            frac_of[g] = frac
             nc.vector.tensor_scalar(
                 out=turns[:], in0=zf, scalar1=INV_TWO_PI, scalar2=phase[:, g:g + 1],
                 op0=ALU.mult, op1=ALU.add,
@@ -205,18 +231,20 @@ def tile_claimencoder_w_kernel(
                 out=frac[:], in0=zf, scalar=INV_TWO_PI, in1=turns[:],
                 op0=ALU.mult, op1=ALU.subtract,
             )
+
+        def trig_s(g):
             nc.scalar.activation(
-                out=fgrp[:, g], in_=frac[:].rearrange("p (t c) -> p c t", t=4),
+                out=fgrp[:, g], in_=frac_of[g][:].rearrange("p (t c) -> p c t", t=4),
                 func=ACTF.Sin, bias=sbias[:, g:g + 1], scale=TWO_PI,
             )
 
         def num(g):
             zb = ztile[g]
-            small_v = rot.tile([P, 4, P], F32, tag="leak", name="leak")
-            nc.scalar.activation(out=small_v[:], in_=zb[:], func=ACTF.Copy, scale=0.01)
+            leak = rot.tile([P, 4, P], F32, tag="leak", name="leak")
+            nc.scalar.activation(out=leak[:], in_=zb[:], func=ACTF.Copy, scale=0.01)
             nc.vector.tensor_tensor(
                 out=fgrp[:, g], in0=zb[:].rearrange("p t c -> p c t"),
-                in1=small_v[:].rearrange("p t c -> p c t"), op=ALU.max,
+                in1=leak[:].rearrange("p t c -> p c t"), op=ALU.max,
             )
 
         def quant_f(g):
@@ -238,13 +266,18 @@ def tile_claimencoder_w_kernel(
                     start=first, stop=last,
                 )
 
-        def bias_bc(layer, i, b):
+        bb_of = {}
+
+        def bias_mm(layer, i, b):
             bb = bank(b, [P, NT], F32, "bb%d_%d" % (layer, i))
+            bb_of[(layer, i)] = bb
             c0 = HID * layer + NT * i
             nc.tensor.matmul(
-                out=bb[:], lhsT=inp[:, 416:544], rhs=brow[:, c0:c0 + NT], start=True, stop=True
+                out=bb[:], lhsT=cst[:, 32:160], rhs=par[:, c0:c0 + NT], start=True, stop=True
             )
-            nc.scalar.copy(out=bbc[:, layer, NT * i:NT * (i + 1)], in_=bb[:])
+
+        def bias_cp(layer, i):
+            nc.scalar.copy(out=bbc[:, layer, NT * i:NT * (i + 1)], in_=bb_of[(layer, i)][:])
 
         def h_epilogue(j):
             pre = rot.tile([P, NT], F32, tag="pre", name="pre")
@@ -256,8 +289,8 @@ def tile_claimencoder_w_kernel(
                 op0=ALU.mult, op1=ALU.max,
             )
 
-        def h_transpose(j, b):
-            xt = bank(b, [P, 8, P], BF16, "xt%d" % j)
+        def h_transpose(j):
+            xt = bank(j, [P, 8, P], BF16, "xt%d" % j)
             for t in range(4):
                 nc.tensor.transpose(
                     out=xt[:, t, :], in_=hb[:, NT * j + t:NT * (j + 1):4], identity=ident[:]
@@ -270,70 +303,76 @@ def tile_claimencoder_w_kernel(
                 in_=hgrp[:, j].rearrange("p c t -> p (c t)"),
             )
 
+        all4 = (0, 1, 2, 3)
         z_block(0)
         z_block(1)
         z_block(2)
+        for i in range(4):
+            bias_mm(0, i, i)
+        trig_v(0)
+        trig_s(0)
+        bias_cp(0, 0)
+        bias_cp(0, 1)
         z_block(3)
-        trig(0)
-        trig(1)
+        trig_v(1)
+        trig_s(1)
         quant_f(0)
+        bias_cp(0, 2)
+        bias_cp(0, 3)
+        for j in range(4):
+            acc1[j] = bank(j, [P, NT], F32, "acc1_%d" % j)
+        l1(0, all4, True, False)
         z_block(4)
-        acc1[0] = bank(0, [P, NT], F32, "acc1_0")
-        acc1[1] = bank(1, [P, NT], F32, "acc1_1")
-        l1(0, (0, 1), True, False)
-        trig(2)
+        trig_v(2)
+        trig_s(2)
         quant_f(1)
-        z_block(5)
-        l1(1, (0, 1), False, False)
-        trig(3)
+        l1(1, all4, False, False)
+        trig_v(3)
+        trig_s(3)
         quant_f(2)
-        z_block(6)
-        l1(2, (0, 1), False, False)
-        trig(4)
+        l1(2, all4, False, False)
+        bias_mm(1, 0, 7)
+        trig_v(4)
+        trig_s(4)
         quant_f(3)
-        z_block(7)
-        l1(3, (0, 1), False, False)
+        bias_cp(1, 0)
+        l1(3, all4, False, False)
+        bias_mm(1, 1, 7)
+        z_block(5)
         num(5)
         quant_f(4)
-        l1(4, (0, 1), False, False)
+        bias_cp(1, 1)
+        l1(4, all4, False, False)
+        bias_mm(1, 2, 7)
+        z_block(6)
+        z_block(7)
         num(6)
         quant_f(5)
+        bias_cp(1, 2)
+        l1(5, all4, False, False)
+        bias_mm(1, 3, 7)
         num(7)
         quant_f(6)
         quant_f(7)
-        for i in range(4):
-            bias_bc(0, i, 6 + i % 2)
-        l1(5, (0, 1), False, False)
+        bias_cp(1, 3)
         l1(6, (0, 1), False, False)
         l1(7, (0, 1), False, True)
-
-        acc1[2] = bank(2, [P, NT], F32, "acc1_2")
-        acc1[3] = bank(3, [P, NT], F32, "acc1_3")
-        h_epilogue(0)
-        h_epilogue(1)
-        l1(0, (2, 3), True, False)
-        l1(1, (2, 3), False, False)
-        h_transpose(0, 6)
-        l1(2, (2, 3), False, False)
-        l1(3, (2, 3), False, False)
-        h_transpose(1, 7)
-        quant_h(0)
-        quant_h(1)
-        l1(4, (2, 3), False, False)
-        l1(5, (2, 3), False, False)
-        for i in range(4):
-            bias_bc(1, i, 6 + i % 2)
         l1(6, (2, 3), False, False)
         l1(7, (2, 3), False, True)
+        h_epilogue(0)
+        h_transpose(0)
+        h_epilogue(1)
+        h_transpose(1)
+        quant_h(0)
         h_epilogue(2)
+        h_transpose(2)
+        quant_h(1)
         h_epilogue(3)
-        h_transpose(2, 6)
-        h_transpose(3, 7)
+        h_transpose(3)
         quant_h(2)
         quant_h(3)
 
-        acc2bank = (4, 5, 0, 1)
-        acc2 = [bank(acc2bank[j], [P, NT], F32, "acc2_%d" % j) for j in range(4)]
+        acc2 = [bank(4 + j, [P, NT], F32, "acc2_%d" % j) for j in range(4)]
 
         def l2(g, j, first, last):
             k = 4 * g

@@ -69,7 +69,7 @@ def tile_claimencoder_w_kernel(
         fcod = keep.tile([P, G1, P], U32, name="fcod", align_bytes=64)
         fscl = keep.tile([P, G1, P], U8, name="fscl", align_bytes=64)
         bbc = keep.tile([P, 2, HID], BF16, name="bbc")
-        hb = keep.tile([P, HID], BF16, name="hb")
+        hb = keep.tile([P, G2, 4, P], BF16, name="hb")
         hgrp = keep.tile([P, G2, P, 4], BF16, name="hgrp", align_bytes=64)
         hcod = keep.tile([P, G2, P], U32, name="hcod", align_bytes=64)
         hscl = keep.tile([P, G2, P], U8, name="hscl", align_bytes=64)
@@ -79,10 +79,14 @@ def tile_claimencoder_w_kernel(
 
         zero(inp_s[:])
         nc.vector.memset(inp_s[0:1, :], 1.0)
-        zero(par[:, 0:2048])
+        zero(par[:, 0:1024])
+        zero(planes[:].rearrange("p a n -> p (a n)"))
+        zero(par[:, 2560:4096])
+        zero(inp_n[:])
+        nc.vector.memset(inp_n[0:1, :], 1.0)
+        zero(par[:, 1024:2560])
         zero(inp_d[:])
         nc.vector.memset(inp_d[32:33, :], 1.0)
-        zero(par[:, 2048:4096])
         zero(cst[:])
         nc.vector.memset(cst[0:1, 0:32], 0.25)
         nc.vector.memset(cst[64:65, 32:160], 1.0)
@@ -90,13 +94,9 @@ def tile_claimencoder_w_kernel(
         nc.vector.memset(
             cosi[0:1, :].rearrange("o (s h c) -> o s h c", h=2, c=80)[:, :, 1, :], 1.0
         )
-        zero(inp_n[:])
-        nc.vector.memset(inp_n[0:1, :], 1.0)
-        nc.vector.memset(warm[:], 0.0)
-        zero(planes[:].rearrange("p a n -> p (a n)"))
+        nc.gpsimd.memset(warm[:], 0.0)
 
         make_identity(nc, ident[:])
-        nc.scalar.activation(out=warm[:, 1:2], in_=warm[:, 0:1], func=ACTF.Sin)
 
         def xy_row(eng, dst, r, xy, which):
             flat = xy.rearrange("(o c) t -> o (c t)", o=1)
@@ -132,61 +132,63 @@ def tile_claimencoder_w_kernel(
                 ].bitcast(I32),
             )
 
-        sy = nc.sync
-        xy_row(sy, inp_s, 1, src_xy, 0)
-        xy_row(sy, inp_s, 2, src_xy, 1)
-        seg_w(sy, 1, 0, src_wsx)
-        seg_b(sy, 0, src_bsx)
-        seg_w(sy, 1, 1, src_wcx)
-        seg_b(sy, 1, src_bcx)
-        sy.dma_start(out=par[64:65, 0:HID], in_=row(b1))
-        seg_w(sy, 2, 2, src_wsy)
-        seg_b(sy, 2, src_bsy)
-        seg_w(sy, 2, 3, src_wcy)
-        seg_b(sy, 3, src_bcy)
-        xy_row(sy, inp_d, 3, dst_xy, 0)
-        xy_row(sy, inp_d, 4, dst_xy, 1)
-        seg_w(sy, 3, 4, dst_wsx)
-        seg_b(sy, 4, dst_bsx)
-        w1_full(0)
-        w1_full(1)
-        scale_tile(0, W1_scales, 0)
-        w1_full(2)
-        sy.dma_start(out=par[64:65, HID:2 * HID], in_=row(b2))
-        w1_full(3)
-        w1_full(4)
-        scale_tile(1, W1_scales, 4)
-        w1_full(5)
-        w1_pair(6, 0)
-        w1_pair(6, 1)
-        scale_tile(2, W2_scales, 0)
-        for g in range(2):
+        sc = nc.scalar
+        gp = nc.gpsimd
+
+        def w2_full(g):
             nc.sync.dma_start(
                 out=w2[:, g, :],
                 in_=W2_words[g].rearrange("p n t -> p (n t)").bitcast(I32),
             )
-        for j in range(4):
+
+        def w2_pair(c0, c1):
             nc.sync.dma_start(
-                out=w2[:, 2:4, NT * j:NT * (j + 1)],
+                out=w2[:, 2:4, c0:c1],
                 in_=W2_words[2:4].rearrange("g p n t -> p g (n t)")[
-                    :, :, 4 * NT * j:4 * NT * (j + 1)
+                    :, :, 4 * c0:4 * c1
                 ].bitcast(I32),
             )
 
-        gp = nc.gpsimd
-        seg_w(gp, 3, 5, dst_wcx)
-        seg_b(gp, 5, dst_bcx)
-        seg_w(gp, 4, 6, dst_wsy)
-        seg_b(gp, 6, dst_bsy)
-        seg_w(gp, 4, 7, dst_wcy)
-        seg_b(gp, 7, dst_bcy)
         nums = ((time_s, t_w, t_b), (wait_src, ws_w, ws_b), (wait_dst, wd_w, wd_b))
+        w1_full(0)
+        w1_full(1)
+        xy_row(sc, inp_s, 1, src_xy, 0)
+        xy_row(sc, inp_s, 2, src_xy, 1)
+        seg_w(sc, 1, 0, src_wsx)
+        seg_b(sc, 0, src_bsx)
+        seg_w(sc, 1, 1, src_wcx)
+        seg_b(sc, 1, src_bcx)
+        nc.scalar.activation(out=warm[:, 1:2], in_=warm[:, 0:1], func=ACTF.Sin)
         for i, (sv, wv, bv) in enumerate(nums):
             gp.dma_start(out=inp_n[5 + i:6 + i, :], in_=row(sv))
         for i, (sv, wv, bv) in enumerate(nums):
             c0 = 2560 + 512 * i
             gp.dma_start(out=par[5 + i:6 + i, c0:c0 + 512], in_=row(wv))
             gp.dma_start(out=par[0:1, c0:c0 + 512], in_=row(bv))
+        w1_full(2)
+        w1_full(3)
+        seg_w(sc, 2, 2, src_wsy)
+        seg_b(sc, 2, src_bsy)
+        seg_w(sc, 2, 3, src_wcy)
+        seg_b(sc, 3, src_bcy)
+        xy_row(sc, inp_d, 3, dst_xy, 0)
+        xy_row(sc, inp_d, 4, dst_xy, 1)
+        scale_tile(0, W1_scales, 0)
+        w1_full(4)
+        w1_full(5)
+        gp.dma_start(out=par[64:65, 0:HID], in_=row(b1))
+        gp.dma_start(out=par[64:65, HID:2 * HID], in_=row(b2))
+        scale_tile(1, W1_scales, 4)
+        w1_pair(6, 0)
+        w1_pair(6, 1)
+        scale_tile(2, W2_scales, 0)
+        w2_full(0)
+        w2_full(1)
+        w2_pair(0, 512)
+        w2_pair(512, 1024)
+        w2_pair(1024, 1536)
+        w2_pair(1536, 1792)
+        w2_pair(1792, 2048)
 
         ph_ps = bank(7, [P, 16, 32], F32, "ph_ps")
         for g in range(TRIG_G):
@@ -279,22 +281,25 @@ def tile_claimencoder_w_kernel(
         def bias_cp(layer, i):
             nc.scalar.copy(out=bbc[:, layer, NT * i:NT * (i + 1)], in_=bb_of[(layer, i)][:])
 
-        def h_epilogue(j):
+        pre_of = {}
+
+        def h_add(j):
             pre = rot.tile([P, NT], F32, tag="pre", name="pre")
+            pre_of[j] = pre
             nc.vector.tensor_tensor(
                 out=pre[:], in0=acc1[j][:], in1=bbc[:, 0, NT * j:NT * (j + 1)], op=ALU.add
             )
+
+        def h_leak(j):
+            pre = pre_of[j][:].rearrange("p (c t) -> p t c", t=4)
             nc.vector.scalar_tensor_tensor(
-                out=hb[:, NT * j:NT * (j + 1)], in0=pre[:], scalar=0.01, in1=pre[:],
-                op0=ALU.mult, op1=ALU.max,
+                out=hb[:, j], in0=pre, scalar=0.01, in1=pre, op0=ALU.mult, op1=ALU.max
             )
 
         def h_transpose(j):
             xt = bank(j, [P, 8, P], BF16, "xt%d" % j)
             for t in range(4):
-                nc.tensor.transpose(
-                    out=xt[:, t, :], in_=hb[:, NT * j + t:NT * (j + 1):4], identity=ident[:]
-                )
+                nc.tensor.transpose(out=xt[:, t, :], in_=hb[:, j, t, :], identity=ident[:])
             nc.scalar.copy(out=hgrp[:, j], in_=xt[:, 0:4, :].rearrange("p t c -> p c t"))
 
         def quant_h(j):
@@ -304,98 +309,110 @@ def tile_claimencoder_w_kernel(
             )
 
         all4 = (0, 1, 2, 3)
-        z_block(0)
-        z_block(1)
-        z_block(2)
-        for i in range(4):
-            bias_mm(0, i, i)
-        trig_v(0)
-        trig_s(0)
-        bias_cp(0, 0)
-        bias_cp(0, 1)
-        z_block(3)
-        trig_v(1)
-        trig_s(1)
-        quant_f(0)
-        bias_cp(0, 2)
-        bias_cp(0, 3)
-        for j in range(4):
+        for j in all4:
             acc1[j] = bank(j, [P, NT], F32, "acc1_%d" % j)
-        l1(0, all4, True, False)
-        z_block(4)
-        trig_v(2)
-        trig_s(2)
+        z_block(0)
+        trig_v(0)
+        z_block(1)
+        trig_v(1)
+        trig_s(0)
+        seg_w(sc, 3, 4, dst_wsx)
+        seg_b(sc, 4, dst_bsx)
+        seg_w(sc, 3, 5, dst_wcx)
+        seg_b(sc, 5, dst_bcx)
+        seg_w(sc, 4, 6, dst_wsy)
+        seg_b(sc, 6, dst_bsy)
+        trig_s(1)
+        seg_w(sc, 4, 7, dst_wcy)
+        seg_b(sc, 7, dst_bcy)
+        quant_f(0)
         quant_f(1)
-        l1(1, all4, False, False)
+        l1(0, all4, True, False)
+        z_block(2)
+        trig_v(2)
+        z_block(3)
         trig_v(3)
+        trig_s(2)
         trig_s(3)
-        quant_f(2)
-        l1(2, all4, False, False)
-        bias_mm(1, 0, 7)
+        l1(1, all4, False, False)
+        z_block(4)
         trig_v(4)
-        trig_s(4)
+        quant_f(2)
         quant_f(3)
-        bias_cp(1, 0)
-        l1(3, all4, False, False)
-        bias_mm(1, 1, 7)
+        trig_s(4)
+        l1(2, all4, False, False)
         z_block(5)
         num(5)
         quant_f(4)
-        bias_cp(1, 1)
-        l1(4, all4, False, False)
-        bias_mm(1, 2, 7)
+        l1(3, all4, False, False)
         z_block(6)
-        z_block(7)
         num(6)
         quant_f(5)
-        bias_cp(1, 2)
-        l1(5, all4, False, False)
-        bias_mm(1, 3, 7)
+        l1(4, all4, False, False)
+        z_block(7)
         num(7)
         quant_f(6)
         quant_f(7)
-        bias_cp(1, 3)
+        l1(5, all4, False, False)
+        for i in range(4):
+            bias_mm(0, i, 6 + i % 2)
+            bias_cp(0, i)
         l1(6, (0, 1), False, False)
         l1(7, (0, 1), False, True)
         l1(6, (2, 3), False, False)
         l1(7, (2, 3), False, True)
-        h_epilogue(0)
+
+        h_add(0)
+        h_add(1)
+        h_leak(0)
+        h_leak(1)
+        for i in range(2):
+            bias_mm(1, i, 6 + i)
+            bias_cp(1, i)
         h_transpose(0)
-        h_epilogue(1)
         h_transpose(1)
+        h_add(2)
         quant_h(0)
-        h_epilogue(2)
-        h_transpose(2)
+        h_add(3)
         quant_h(1)
-        h_epilogue(3)
+        h_leak(2)
+        h_leak(3)
+        for i in range(2, 4):
+            bias_mm(1, i, 4 + i)
+            bias_cp(1, i)
+        h_transpose(2)
         h_transpose(3)
         quant_h(2)
         quant_h(3)
 
-        acc2 = [bank(4 + j, [P, NT], F32, "acc2_%d" % j) for j in range(4)]
+        cols = ((0, 512, 4), (512, 1024, 5), (1024, 1536, 6), (1536, 1792, 7), (1792, 2048, 0))
+        acc2 = [bank(b, [P, c1 - c0], F32, "acc2_%d" % c0) for c0, c1, b in cols]
 
-        def l2(g, j, first, last):
+        def l2(g, i, first, last):
             k = 4 * g
+            c0, c1, b = cols[i]
             nc.tensor.matmul_mx(
-                out=acc2[j][:],
+                out=acc2[i][:],
                 lhsT=hcod[:, g, :].bitcast(FP8X4), lhsT_scale=hscl[:, g, :],
-                rhs=w2[:, g, NT * j:NT * (j + 1)].bitcast(FP8X4),
-                rhs_scale=planes[k:P, 2, NT * j:NT * (j + 1)],
+                rhs=w2[:, g, c0:c1].bitcast(FP8X4),
+                rhs_scale=planes[k:P, 2, c0:c1],
                 start=first, stop=last,
             )
 
         for g in range(2):
-            for j in range(4):
-                l2(g, j, g == 0, False)
-        for j in range(4):
-            l2(2, j, False, False)
-            l2(3, j, False, True)
+            for i in range(len(cols)):
+                l2(g, i, g == 0, False)
+        for i, (c0, c1, b) in enumerate(cols):
+            l2(2, i, False, False)
+            l2(3, i, False, True)
             pre = rot.tile([P, NT], F32, tag="pre", name="pre")
             res = outp.tile([P, NT], F32, tag="res", name="res")
+            n = c1 - c0
             nc.vector.tensor_tensor(
-                out=pre[:], in0=acc2[j][:], in1=bbc[:, 1, NT * j:NT * (j + 1)], op=ALU.add
+                out=pre[:, 0:n], in0=acc2[i][:], in1=bbc[:, 1, c0:c1], op=ALU.add
             )
             nc.vector.scalar_tensor_tensor(
-                out=res[:], in0=pre[:], scalar=0.01, in1=pre[:], op0=ALU.mult, op1=ALU.max
+                out=res[:, 0:n], in0=pre[:, 0:n], scalar=0.01, in1=pre[:, 0:n],
+                op0=ALU.mult, op1=ALU.max,
             )
-            nc.sync.dma_start(out=out[:, NT * j:NT * (j + 1)], in_=res[:])
+            nc.sync.dma_start(out=out[:, c0:c1], in_=res[:, 0:n])

@@ -56,7 +56,8 @@ def tile_claimencoder_w_kernel(
         inp_s = keep.tile([P, 256], BF16, name="inp_s")
         inp_d = keep.tile([P, 256], BF16, name="inp_d")
         inp_n = keep.tile([P, P], BF16, name="inp_n")
-        cst = keep.tile([P, 160], BF16, name="cst")
+        cst = keep.tile([P, 288], BF16, name="cst")
+        bpar = keep.tile([P, HID], BF16, name="bpar")
         cosi = keep.tile([P, 640], BF16, name="cosi")
         warm = keep.tile([P, 2], F32, name="warm")
         ident = keep.tile([P, P], BF16, name="ident")
@@ -68,7 +69,8 @@ def tile_claimencoder_w_kernel(
         fgrp = keep.tile([P, G1, P, 4], BF16, name="fgrp", align_bytes=64)
         fcod = keep.tile([P, G1, P], U32, name="fcod", align_bytes=64)
         fscl = keep.tile([P, G1, P], U8, name="fscl", align_bytes=64)
-        bbc = keep.tile([P, 2, HID], BF16, name="bbc")
+        bbh = keep.tile([P, G2, 4, P], BF16, name="bbh")
+        bbo = keep.tile([P, HID], BF16, name="bbo")
         hb = keep.tile([P, G2, 4, P], BF16, name="hb")
         hgrp = keep.tile([P, G2, P, 4], BF16, name="hgrp", align_bytes=64)
         hcod = keep.tile([P, G2, P], U32, name="hcod", align_bytes=64)
@@ -79,24 +81,28 @@ def tile_claimencoder_w_kernel(
 
         zero(inp_s[:])
         nc.vector.memset(inp_s[0:1, :], 1.0)
-        zero(par[:, 0:1024])
-        zero(planes[:].rearrange("p a n -> p (a n)"))
-        zero(par[:, 2560:4096])
+        zero(par[:, 0:640])
         zero(inp_n[:])
         nc.vector.memset(inp_n[0:1, :], 1.0)
-        zero(par[:, 1024:2560])
+        zero(par[:, 2560:4096])
+        zero(par[:, 640:1280])
         zero(inp_d[:])
         nc.vector.memset(inp_d[32:33, :], 1.0)
+        zero(planes[:].rearrange("p a n -> p (a n)"))
+        zero(par[:, 1280:2560])
         zero(cst[:])
         nc.vector.memset(cst[0:1, 0:32], 0.25)
-        nc.vector.memset(cst[64:65, 32:160], 1.0)
         zero(cosi[:])
         nc.vector.memset(
             cosi[0:1, :].rearrange("o (s h c) -> o s h c", h=2, c=80)[:, :, 1, :], 1.0
         )
+        zero(bpar[:])
+        nc.vector.memset(cst[0:1, 32:160], 1.0)
+        nc.vector.memset(cst[32:33, 160:288], 1.0)
         nc.gpsimd.memset(warm[:], 0.0)
 
         make_identity(nc, ident[:])
+        nc.scalar.activation(out=warm[:, 1:2], in_=warm[:, 0:1], func=ACTF.Sin)
 
         def xy_row(eng, dst, r, xy, which):
             flat = xy.rearrange("(o c) t -> o (c t)", o=1)
@@ -124,6 +130,14 @@ def tile_claimencoder_w_kernel(
                 out=w1[:, g, :], in_=W1_words[g].rearrange("p n t -> p (n t)").bitcast(I32)
             )
 
+        def w1_half(g, h):
+            nc.sync.dma_start(
+                out=w1[:, g, 1024 * h:1024 * (h + 1)],
+                in_=W1_words[g].rearrange("p n t -> p (n t)")[
+                    :, 4096 * h:4096 * (h + 1)
+                ].bitcast(I32),
+            )
+
         def w1_pair(g, h):
             nc.sync.dma_start(
                 out=w1[:, g:g + 2, 1024 * h:1024 * (h + 1)],
@@ -132,7 +146,6 @@ def tile_claimencoder_w_kernel(
                 ].bitcast(I32),
             )
 
-        sc = nc.scalar
         gp = nc.gpsimd
 
         def w2_full(g):
@@ -149,38 +162,39 @@ def tile_claimencoder_w_kernel(
                 ].bitcast(I32),
             )
 
-        nums = ((time_s, t_w, t_b), (wait_src, ws_w, ws_b), (wait_dst, wd_w, wd_b))
-        w1_full(0)
-        w1_full(1)
-        xy_row(sc, inp_s, 1, src_xy, 0)
-        xy_row(sc, inp_s, 2, src_xy, 1)
-        seg_w(sc, 1, 0, src_wsx)
-        seg_b(sc, 0, src_bsx)
-        seg_w(sc, 1, 1, src_wcx)
-        seg_b(sc, 1, src_bcx)
-        nc.scalar.activation(out=warm[:, 1:2], in_=warm[:, 0:1], func=ACTF.Sin)
-        for i, (sv, wv, bv) in enumerate(nums):
-            gp.dma_start(out=inp_n[5 + i:6 + i, :], in_=row(sv))
-        for i, (sv, wv, bv) in enumerate(nums):
-            c0 = 2560 + 512 * i
-            gp.dma_start(out=par[5 + i:6 + i, c0:c0 + 512], in_=row(wv))
-            gp.dma_start(out=par[0:1, c0:c0 + 512], in_=row(bv))
-        w1_full(2)
-        w1_full(3)
-        seg_w(sc, 2, 2, src_wsy)
-        seg_b(sc, 2, src_bsy)
-        seg_w(sc, 2, 3, src_wcy)
-        seg_b(sc, 3, src_bcy)
-        xy_row(sc, inp_d, 3, dst_xy, 0)
-        xy_row(sc, inp_d, 4, dst_xy, 1)
+        sy = nc.sync
+        xy_row(sy, inp_s, 1, src_xy, 0)
+        xy_row(sy, inp_s, 2, src_xy, 1)
+        seg_w(sy, 1, 0, src_wsx)
+        seg_b(sy, 0, src_bsx)
+        seg_w(sy, 1, 1, src_wcx)
+        seg_b(sy, 1, src_bcx)
+        w1_half(0, 0)
+        w1_half(0, 1)
+        seg_w(sy, 2, 2, src_wsy)
+        seg_b(sy, 2, src_bsy)
+        seg_w(sy, 2, 3, src_wcy)
+        seg_b(sy, 3, src_bcy)
+        xy_row(sy, inp_d, 3, dst_xy, 0)
+        xy_row(sy, inp_d, 4, dst_xy, 1)
+        w1_half(1, 0)
+        w1_half(1, 1)
+        seg_w(sy, 3, 4, dst_wsx)
+        seg_b(sy, 4, dst_bsx)
         scale_tile(0, W1_scales, 0)
-        w1_full(4)
+        w1_full(2)
         w1_full(5)
-        gp.dma_start(out=par[64:65, 0:HID], in_=row(b1))
-        gp.dma_start(out=par[64:65, HID:2 * HID], in_=row(b2))
+        seg_w(sy, 3, 5, dst_wcx)
+        seg_b(sy, 5, dst_bcx)
         scale_tile(1, W1_scales, 4)
-        w1_pair(6, 0)
-        w1_pair(6, 1)
+        w1_full(6)
+        w1_full(7)
+        seg_w(sy, 4, 6, dst_wsy)
+        seg_b(sy, 6, dst_bsy)
+        seg_w(sy, 4, 7, dst_wcy)
+        seg_b(sy, 7, dst_bcy)
+        w1_pair(3, 0)
+        w1_pair(3, 1)
         scale_tile(2, W2_scales, 0)
         w2_full(0)
         w2_full(1)
@@ -189,6 +203,16 @@ def tile_claimencoder_w_kernel(
         w2_pair(1024, 1536)
         w2_pair(1536, 1792)
         w2_pair(1792, 2048)
+
+        nums = ((time_s, t_w, t_b), (wait_src, ws_w, ws_b), (wait_dst, wd_w, wd_b))
+        for i, (sv, wv, bv) in enumerate(nums):
+            gp.dma_start(out=inp_n[5 + i:6 + i, :], in_=row(sv))
+        for i, (sv, wv, bv) in enumerate(nums):
+            c0 = 2560 + 512 * i
+            gp.dma_start(out=par[5 + i:6 + i, c0:c0 + 512], in_=row(wv))
+            gp.dma_start(out=par[0:1, c0:c0 + 512], in_=row(bv))
+        gp.dma_start(out=bpar[0:1, :], in_=row(b1))
+        gp.dma_start(out=bpar[32:33, :], in_=row(b2))
 
         ph_ps = bank(7, [P, 16, 32], F32, "ph_ps")
         for g in range(TRIG_G):
@@ -201,7 +225,7 @@ def tile_claimencoder_w_kernel(
             out=sbias[:], in0=ph_ps[:, 0:TRIG_G, 0], scalar1=TWO_PI, scalar2=None, op0=ALU.mult
         )
 
-        zbank = {0: 4, 1: 5, 2: 6, 3: 4, 4: 5, 5: 6, 6: 4, 7: 5}
+        zbank = {0: 4, 1: 5, 2: 6, 5: 4, 6: 5, 3: 6, 4: 4, 7: 5}
         zrhs = {0: (inp_s,), 1: (inp_s,), 2: (inp_s, inp_d), 3: (inp_d,), 4: (inp_d,)}
         ztile = {}
         frac_of = {}
@@ -273,25 +297,30 @@ def tile_claimencoder_w_kernel(
         def bias_mm(layer, i, b):
             bb = bank(b, [P, NT], F32, "bb%d_%d" % (layer, i))
             bb_of[(layer, i)] = bb
-            c0 = HID * layer + NT * i
             nc.tensor.matmul(
-                out=bb[:], lhsT=cst[:, 32:160], rhs=par[:, c0:c0 + NT], start=True, stop=True
+                out=bb[:], lhsT=cst[:, 32 + P * layer:32 + P * (layer + 1)],
+                rhs=bpar[:, NT * i:NT * (i + 1)], start=True, stop=True,
             )
 
         def bias_cp(layer, i):
-            nc.scalar.copy(out=bbc[:, layer, NT * i:NT * (i + 1)], in_=bb_of[(layer, i)][:])
+            bb = bb_of[(layer, i)]
+            if layer == 0:
+                nc.scalar.copy(out=bbh[:, i], in_=bb[:].rearrange("p (c t) -> p t c", t=4))
+            else:
+                nc.scalar.copy(out=bbo[:, NT * i:NT * (i + 1)], in_=bb[:])
 
         pre_of = {}
 
         def h_add(j):
-            pre = rot.tile([P, NT], F32, tag="pre", name="pre")
+            pre = rot.tile([P, 4, P], F32, tag="pre", name="pre")
             pre_of[j] = pre
             nc.vector.tensor_tensor(
-                out=pre[:], in0=acc1[j][:], in1=bbc[:, 0, NT * j:NT * (j + 1)], op=ALU.add
+                out=pre[:], in0=acc1[j][:].rearrange("p (c t) -> p t c", t=4),
+                in1=bbh[:, j], op=ALU.add,
             )
 
         def h_leak(j):
-            pre = pre_of[j][:].rearrange("p (c t) -> p t c", t=4)
+            pre = pre_of[j][:]
             nc.vector.scalar_tensor_tensor(
                 out=hb[:, j], in0=pre, scalar=0.01, in1=pre, op0=ALU.mult, op1=ALU.max
             )
@@ -313,54 +342,46 @@ def tile_claimencoder_w_kernel(
             acc1[j] = bank(j, [P, NT], F32, "acc1_%d" % j)
         z_block(0)
         trig_v(0)
+        trig_s(0)
         z_block(1)
         trig_v(1)
-        trig_s(0)
-        seg_w(sc, 3, 4, dst_wsx)
-        seg_b(sc, 4, dst_bsx)
-        seg_w(sc, 3, 5, dst_wcx)
-        seg_b(sc, 5, dst_bcx)
-        seg_w(sc, 4, 6, dst_wsy)
-        seg_b(sc, 6, dst_bsy)
-        trig_s(1)
-        seg_w(sc, 4, 7, dst_wcy)
-        seg_b(sc, 7, dst_bcy)
         quant_f(0)
-        quant_f(1)
-        l1(0, all4, True, False)
+        trig_s(1)
         z_block(2)
+        l1(0, all4, True, False)
         trig_v(2)
-        z_block(3)
-        trig_v(3)
+        quant_f(1)
         trig_s(2)
-        trig_s(3)
-        l1(1, all4, False, False)
-        z_block(4)
-        trig_v(4)
-        quant_f(2)
-        quant_f(3)
-        trig_s(4)
-        l1(2, all4, False, False)
         z_block(5)
+        l1(1, all4, False, False)
         num(5)
-        quant_f(4)
-        l1(3, all4, False, False)
+        quant_f(2)
         z_block(6)
+        l1(2, all4, False, False)
         num(6)
         quant_f(5)
-        l1(4, all4, False, False)
+        z_block(3)
+        l1(5, all4, False, False)
+        trig_v(3)
+        quant_f(6)
+        trig_s(3)
+        z_block(4)
+        l1(6, all4, False, False)
+        trig_v(4)
+        quant_f(3)
+        trig_s(4)
         z_block(7)
         num(7)
-        quant_f(6)
+        quant_f(4)
         quant_f(7)
-        l1(5, all4, False, False)
         for i in range(4):
             bias_mm(0, i, 6 + i % 2)
             bias_cp(0, i)
-        l1(6, (0, 1), False, False)
-        l1(7, (0, 1), False, True)
-        l1(6, (2, 3), False, False)
-        l1(7, (2, 3), False, True)
+        l1(7, all4, False, False)
+        l1(3, (0, 1), False, False)
+        l1(4, (0, 1), False, True)
+        l1(3, (2, 3), False, False)
+        l1(4, (2, 3), False, True)
 
         h_add(0)
         h_add(1)
@@ -405,11 +426,11 @@ def tile_claimencoder_w_kernel(
         for i, (c0, c1, b) in enumerate(cols):
             l2(2, i, False, False)
             l2(3, i, False, True)
-            pre = rot.tile([P, NT], F32, tag="pre", name="pre")
+            pre = rot.tile([P, NT], F32, tag="preo", name="preo")
             res = outp.tile([P, NT], F32, tag="res", name="res")
             n = c1 - c0
             nc.vector.tensor_tensor(
-                out=pre[:, 0:n], in0=acc2[i][:], in1=bbc[:, 1, c0:c1], op=ALU.add
+                out=pre[:, 0:n], in0=acc2[i][:], in1=bbo[:, c0:c1], op=ALU.add
             )
             nc.vector.scalar_tensor_tensor(
                 out=res[:, 0:n], in0=pre[:, 0:n], scalar=0.01, in1=pre[:, 0:n],

@@ -130,14 +130,6 @@ def tile_claimencoder_w_kernel(
                 out=w1[:, g, :], in_=W1_words[g].rearrange("p n t -> p (n t)").bitcast(I32)
             )
 
-        def w1_half(g, h):
-            nc.sync.dma_start(
-                out=w1[:, g, 1024 * h:1024 * (h + 1)],
-                in_=W1_words[g].rearrange("p n t -> p (n t)")[
-                    :, 4096 * h:4096 * (h + 1)
-                ].bitcast(I32),
-            )
-
         def w1_pair(g, h):
             nc.sync.dma_start(
                 out=w1[:, g:g + 2, 1024 * h:1024 * (h + 1)],
@@ -162,37 +154,35 @@ def tile_claimencoder_w_kernel(
                 ].bitcast(I32),
             )
 
-        sy = nc.sync
-        xy_row(sy, inp_s, 1, src_xy, 0)
-        xy_row(sy, inp_s, 2, src_xy, 1)
-        seg_w(sy, 1, 0, src_wsx)
-        seg_b(sy, 0, src_bsx)
-        seg_w(sy, 1, 1, src_wcx)
-        seg_b(sy, 1, src_bcx)
-        w1_half(0, 0)
-        w1_half(0, 1)
-        seg_w(sy, 2, 2, src_wsy)
-        seg_b(sy, 2, src_bsy)
-        seg_w(sy, 2, 3, src_wcy)
-        seg_b(sy, 3, src_bcy)
-        xy_row(sy, inp_d, 3, dst_xy, 0)
-        xy_row(sy, inp_d, 4, dst_xy, 1)
-        w1_half(1, 0)
-        w1_half(1, 1)
-        seg_w(sy, 3, 4, dst_wsx)
-        seg_b(sy, 4, dst_bsx)
+        sc = nc.scalar
+        w1_full(0)
+        xy_row(sc, inp_s, 1, src_xy, 0)
+        xy_row(sc, inp_s, 2, src_xy, 1)
+        seg_w(sc, 1, 0, src_wsx)
+        seg_b(sc, 0, src_bsx)
+        seg_w(sc, 1, 1, src_wcx)
+        seg_b(sc, 1, src_bcx)
+        w1_full(1)
+        seg_w(sc, 2, 2, src_wsy)
+        seg_b(sc, 2, src_bsy)
+        seg_w(sc, 2, 3, src_wcy)
+        seg_b(sc, 3, src_bcy)
+        xy_row(sc, inp_d, 3, dst_xy, 0)
+        xy_row(sc, inp_d, 4, dst_xy, 1)
         scale_tile(0, W1_scales, 0)
         w1_full(2)
-        w1_full(5)
-        seg_w(sy, 3, 5, dst_wcx)
-        seg_b(sy, 5, dst_bcx)
+        seg_w(sc, 3, 4, dst_wsx)
+        seg_b(sc, 4, dst_bsx)
+        seg_w(sc, 3, 5, dst_wcx)
+        seg_b(sc, 5, dst_bcx)
         scale_tile(1, W1_scales, 4)
+        w1_full(5)
+        seg_w(sc, 4, 6, dst_wsy)
+        seg_b(sc, 6, dst_bsy)
+        seg_w(sc, 4, 7, dst_wcy)
+        seg_b(sc, 7, dst_bcy)
         w1_full(6)
         w1_full(7)
-        seg_w(sy, 4, 6, dst_wsy)
-        seg_b(sy, 6, dst_bsy)
-        seg_w(sy, 4, 7, dst_wcy)
-        seg_b(sy, 7, dst_bcy)
         w1_pair(3, 0)
         w1_pair(3, 1)
         scale_tile(2, W2_scales, 0)

@@ -46,6 +46,7 @@ def tile_claimencoder_w_kernel(
         ctx.enter_context(tc.manual_schedule())
         keep = ctx.enter_context(tc.tile_pool(name="keep", bufs=1))
         rot = ctx.enter_context(tc.tile_pool(name="rot", bufs=2))
+        frp = ctx.enter_context(tc.tile_pool(name="frp", bufs=5))
         outp = ctx.enter_context(tc.tile_pool(name="outp", bufs=4))
         ps = ctx.enter_context(tc.psum_pool(name="ps", bufs=1))
 
@@ -81,28 +82,30 @@ def tile_claimencoder_w_kernel(
 
         zero(inp_s[:])
         nc.vector.memset(inp_s[0:1, :], 1.0)
+        zero(planes[:, 0, :])
         zero(par[:, 0:640])
-        zero(inp_n[:])
-        nc.vector.memset(inp_n[0:1, :], 1.0)
-        zero(par[:, 2560:4096])
         zero(par[:, 640:1280])
-        zero(inp_d[:])
-        nc.vector.memset(inp_d[32:33, :], 1.0)
-        zero(planes[:].rearrange("p a n -> p (a n)"))
-        zero(par[:, 1280:2560])
         zero(cst[:])
         nc.vector.memset(cst[0:1, 0:32], 0.25)
         zero(cosi[:])
         nc.vector.memset(
             cosi[0:1, :].rearrange("o (s h c) -> o s h c", h=2, c=80)[:, :, 1, :], 1.0
         )
-        zero(bpar[:])
+        zero(planes[:, 1, :])
+        zero(planes[:, 2, :])
         nc.vector.memset(cst[0:1, 32:160], 1.0)
         nc.vector.memset(cst[32:33, 160:288], 1.0)
-        nc.gpsimd.memset(warm[:], 0.0)
 
-        make_identity(nc, ident[:])
-        nc.scalar.activation(out=warm[:, 1:2], in_=warm[:, 0:1], func=ACTF.Sin)
+        def gzero(ap):
+            nc.gpsimd.memset(ap.bitcast(I32), 0)
+
+        gzero(inp_d[:])
+        nc.gpsimd.memset(inp_d[32:33, :], 1.0)
+        gzero(par[:, 1280:2560])
+        gzero(inp_n[:])
+        nc.gpsimd.memset(inp_n[0:1, :], 1.0)
+        gzero(par[:, 2560:4096])
+        nc.gpsimd.memset(warm[:], 0.0)
 
         def xy_row(eng, dst, r, xy, which):
             flat = xy.rearrange("(o c) t -> o (c t)", o=1)
@@ -118,23 +121,22 @@ def tile_claimencoder_w_kernel(
             r = 0 if s < 4 else 32
             eng.dma_start(out=par[r:r + 1, SEG * s:SEG * (s + 1)], in_=row(bv))
 
-        def scale_tile(a, scales, g0):
-            for q in range(4):
-                nc.sync.dma_start(
-                    out=planes[32 * q:32 * q + 16, a, :].bitcast(I32),
-                    in_=scales[g0:g0 + 4, 4 * q:4 * q + 4, :].bitcast(I32),
-                )
+        def scale_q(a, scales, g0, q):
+            nc.sync.dma_start(
+                out=planes[32 * q:32 * q + 16, a, :].bitcast(I32),
+                in_=scales[g0:g0 + 4, 4 * q:4 * q + 4, :].bitcast(I32),
+            )
 
         def w1_full(g):
             nc.sync.dma_start(
                 out=w1[:, g, :], in_=W1_words[g].rearrange("p n t -> p (n t)").bitcast(I32)
             )
 
-        def w1_pair(g, h):
+        def w1_pair(g, j):
             nc.sync.dma_start(
-                out=w1[:, g:g + 2, 1024 * h:1024 * (h + 1)],
+                out=w1[:, g:g + 2, NT * j:NT * (j + 1)],
                 in_=W1_words[g:g + 2].rearrange("g p n t -> p g (n t)")[
-                    :, :, 4096 * h:4096 * (h + 1)
+                    :, :, 4 * NT * j:4 * NT * (j + 1)
                 ].bitcast(I32),
             )
 
@@ -154,38 +156,16 @@ def tile_claimencoder_w_kernel(
                 ].bitcast(I32),
             )
 
-        sc = nc.scalar
-        w1_full(0)
-        xy_row(sc, inp_s, 1, src_xy, 0)
-        xy_row(sc, inp_s, 2, src_xy, 1)
-        seg_w(sc, 1, 0, src_wsx)
-        seg_b(sc, 0, src_bsx)
-        seg_w(sc, 1, 1, src_wcx)
-        seg_b(sc, 1, src_bcx)
-        w1_full(1)
-        seg_w(sc, 2, 2, src_wsy)
-        seg_b(sc, 2, src_bsy)
-        seg_w(sc, 2, 3, src_wcy)
-        seg_b(sc, 3, src_bcy)
-        xy_row(sc, inp_d, 3, dst_xy, 0)
-        xy_row(sc, inp_d, 4, dst_xy, 1)
-        scale_tile(0, W1_scales, 0)
-        w1_full(2)
-        seg_w(sc, 3, 4, dst_wsx)
-        seg_b(sc, 4, dst_bsx)
-        seg_w(sc, 3, 5, dst_wcx)
-        seg_b(sc, 5, dst_bcx)
-        scale_tile(1, W1_scales, 4)
-        w1_full(5)
-        seg_w(sc, 4, 6, dst_wsy)
-        seg_b(sc, 6, dst_bsy)
-        seg_w(sc, 4, 7, dst_wcy)
-        seg_b(sc, 7, dst_bcy)
-        w1_full(6)
-        w1_full(7)
-        w1_pair(3, 0)
-        w1_pair(3, 1)
-        scale_tile(2, W2_scales, 0)
+        for q in range(4):
+            scale_q(0, W1_scales, 0, q)
+        for g in (0, 1, 2, 5, 6, 7):
+            w1_full(g)
+        for q in range(4):
+            scale_q(1, W1_scales, 4, q)
+        for j in range(4):
+            w1_pair(3, j)
+        for q in range(4):
+            scale_q(2, W2_scales, 0, q)
         w2_full(0)
         w2_full(1)
         w2_pair(0, 512)
@@ -194,15 +174,39 @@ def tile_claimencoder_w_kernel(
         w2_pair(1536, 1792)
         w2_pair(1792, 2048)
 
+        sc = nc.scalar
+        xy_row(sc, inp_s, 1, src_xy, 0)
+        xy_row(sc, inp_s, 2, src_xy, 1)
+        xy_row(sc, inp_d, 3, dst_xy, 0)
+        xy_row(sc, inp_d, 4, dst_xy, 1)
+        seg_w(sc, 1, 0, src_wsx)
+        seg_b(sc, 0, src_bsx)
+        seg_w(sc, 1, 1, src_wcx)
+        seg_b(sc, 1, src_bcx)
+        seg_w(sc, 2, 2, src_wsy)
+        seg_b(sc, 2, src_bsy)
+        seg_w(sc, 2, 3, src_wcy)
+        seg_b(sc, 3, src_bcy)
+        seg_w(sc, 3, 4, dst_wsx)
+        seg_b(sc, 4, dst_bsx)
+        seg_w(sc, 3, 5, dst_wcx)
+        seg_b(sc, 5, dst_bcx)
+        seg_w(sc, 4, 6, dst_wsy)
+        seg_b(sc, 6, dst_bsy)
+        seg_w(sc, 4, 7, dst_wcy)
+        seg_b(sc, 7, dst_bcy)
+        nc.scalar.activation(out=warm[:, 1:2], in_=warm[:, 0:1], func=ACTF.Sin)
+
         nums = ((time_s, t_w, t_b), (wait_src, ws_w, ws_b), (wait_dst, wd_w, wd_b))
         for i, (sv, wv, bv) in enumerate(nums):
-            gp.dma_start(out=inp_n[5 + i:6 + i, :], in_=row(sv))
-        for i, (sv, wv, bv) in enumerate(nums):
             c0 = 2560 + 512 * i
+            gp.dma_start(out=inp_n[5 + i:6 + i, :], in_=row(sv))
             gp.dma_start(out=par[5 + i:6 + i, c0:c0 + 512], in_=row(wv))
             gp.dma_start(out=par[0:1, c0:c0 + 512], in_=row(bv))
+        gzero(bpar[:])
         gp.dma_start(out=bpar[0:1, :], in_=row(b1))
         gp.dma_start(out=bpar[32:33, :], in_=row(b2))
+        make_identity(nc, ident[:])
 
         ph_ps = bank(7, [P, 16, 32], F32, "ph_ps")
         for g in range(TRIG_G):
@@ -215,7 +219,7 @@ def tile_claimencoder_w_kernel(
             out=sbias[:], in0=ph_ps[:, 0:TRIG_G, 0], scalar1=TWO_PI, scalar2=None, op0=ALU.mult
         )
 
-        zbank = {0: 4, 1: 5, 2: 6, 5: 4, 6: 5, 3: 6, 4: 4, 7: 5}
+        zbank = {0: 4, 1: 5, 5: 7, 2: 6, 6: 4, 3: 5, 7: 6, 4: 7}
         zrhs = {0: (inp_s,), 1: (inp_s,), 2: (inp_s, inp_d), 3: (inp_d,), 4: (inp_d,)}
         ztile = {}
         frac_of = {}
@@ -237,7 +241,7 @@ def tile_claimencoder_w_kernel(
         def trig_v(g):
             zf = ztile[g][:].rearrange("p t c -> p (t c)")
             turns = rot.tile([P, NT], I32, tag="turns", name="turns")
-            frac = rot.tile([P, NT], F32, tag="frac", name="frac")
+            frac = frp.tile([P, NT], F32, tag="frac", name="frac")
             frac_of[g] = frac
             nc.vector.tensor_scalar(
                 out=turns[:], in0=zf, scalar1=INV_TWO_PI, scalar2=phase[:, g:g + 1],
@@ -335,65 +339,61 @@ def tile_claimencoder_w_kernel(
         trig_s(0)
         z_block(1)
         trig_v(1)
+        z_block(5)
+        num(5)
         quant_f(0)
         trig_s(1)
         z_block(2)
-        l1(0, all4, True, False)
         trig_v(2)
+        z_block(6)
+        num(6)
         quant_f(1)
         trig_s(2)
-        z_block(5)
-        l1(1, all4, False, False)
-        num(5)
-        quant_f(2)
-        z_block(6)
-        l1(2, all4, False, False)
-        num(6)
+        l1(0, all4, True, False)
         quant_f(5)
         z_block(3)
-        l1(5, all4, False, False)
         trig_v(3)
-        quant_f(6)
         trig_s(3)
-        z_block(4)
-        l1(6, all4, False, False)
-        trig_v(4)
-        quant_f(3)
-        trig_s(4)
+        l1(1, all4, False, False)
+        quant_f(2)
+        quant_f(6)
         z_block(7)
         num(7)
-        quant_f(4)
+        z_block(4)
+        trig_v(4)
+        trig_s(4)
+        l1(2, all4, False, False)
+        quant_f(3)
         quant_f(7)
+        l1(5, all4, False, False)
+        quant_f(4)
+        l1(6, all4, False, False)
         for i in range(4):
-            bias_mm(0, i, 6 + i % 2)
+            bias_mm(0, i, 4 + i % 2)
             bias_cp(0, i)
         l1(7, all4, False, False)
-        l1(3, (0, 1), False, False)
-        l1(4, (0, 1), False, True)
-        l1(3, (2, 3), False, False)
-        l1(4, (2, 3), False, True)
-
+        for j in range(2):
+            l1(3, (j,), False, False)
+            l1(4, (j,), False, True)
         h_add(0)
-        h_add(1)
         h_leak(0)
-        h_leak(1)
-        for i in range(2):
-            bias_mm(1, i, 6 + i)
-            bias_cp(1, i)
         h_transpose(0)
-        h_transpose(1)
-        h_add(2)
+        l1(3, (2,), False, False)
+        l1(4, (2,), False, True)
+        h_add(1)
+        h_leak(1)
         quant_h(0)
-        h_add(3)
-        quant_h(1)
+        h_transpose(1)
+        l1(3, (3,), False, False)
+        l1(4, (3,), False, True)
+        h_add(2)
         h_leak(2)
-        h_leak(3)
-        for i in range(2, 4):
-            bias_mm(1, i, 4 + i)
-            bias_cp(1, i)
+        quant_h(1)
         h_transpose(2)
-        h_transpose(3)
+        h_add(3)
+        h_leak(3)
         quant_h(2)
+        h_transpose(3)
         quant_h(3)
 
         cols = ((0, 512, 4), (512, 1024, 5), (1024, 1536, 6), (1536, 1792, 7), (1792, 2048, 0))
@@ -410,9 +410,13 @@ def tile_claimencoder_w_kernel(
                 start=first, stop=last,
             )
 
-        for g in range(2):
-            for i in range(len(cols)):
-                l2(g, i, g == 0, False)
+        for i in range(len(cols)):
+            l2(0, i, True, False)
+        for i in range(4):
+            bias_mm(1, i, 1 + i % 2)
+            bias_cp(1, i)
+        for i in range(len(cols)):
+            l2(1, i, False, False)
         for i, (c0, c1, b) in enumerate(cols):
             l2(2, i, False, False)
             l2(3, i, False, True)

@@ -56,7 +56,7 @@ def tile_claimencoder_w_kernel(
         par = keep.tile([P, FEAT], BF16, name="par")
         inp_s = keep.tile([P, 256], BF16, name="inp_s")
         inp_d = keep.tile([P, 256], BF16, name="inp_d")
-        inp_n = keep.tile([P, P], BF16, name="inp_n")
+        inp_n = keep.tile([P, 3, P], BF16, name="inp_n")
         cst = keep.tile([P, 288], BF16, name="cst")
         bpar = keep.tile([P, HID], BF16, name="bpar")
         cosi = keep.tile([P, 640], BF16, name="cosi")
@@ -82,30 +82,30 @@ def tile_claimencoder_w_kernel(
 
         zero(inp_s[:])
         nc.vector.memset(inp_s[0:1, :], 1.0)
-        zero(planes[:, 0, :])
         zero(par[:, 0:640])
         zero(par[:, 640:1280])
+        zero(inp_d[:])
+        nc.vector.memset(inp_d[32:33, :], 1.0)
+        zero(par[:, 1280:1920])
         zero(cst[:])
         nc.vector.memset(cst[0:1, 0:32], 0.25)
         zero(cosi[:])
         nc.vector.memset(
             cosi[0:1, :].rearrange("o (s h c) -> o s h c", h=2, c=80)[:, :, 1, :], 1.0
         )
-        zero(planes[:, 1, :])
-        zero(planes[:, 2, :])
+        zero(planes[:, 0, :])
         nc.vector.memset(cst[0:1, 32:160], 1.0)
         nc.vector.memset(cst[32:33, 160:288], 1.0)
 
         def gzero(ap):
             nc.gpsimd.memset(ap.bitcast(I32), 0)
 
-        gzero(inp_d[:])
-        nc.gpsimd.memset(inp_d[32:33, :], 1.0)
-        gzero(par[:, 1280:2560])
-        gzero(inp_n[:])
-        nc.gpsimd.memset(inp_n[0:1, :], 1.0)
-        gzero(par[:, 2560:4096])
         nc.gpsimd.memset(warm[:], 0.0)
+        gzero(par[:, 1920:2560])
+        gzero(inp_n[:].rearrange("p i c -> p (i c)"))
+        nc.gpsimd.memset(inp_n[0:1, :, :], 1.0)
+        gzero(par[:, 2560:4096])
+        nc.scalar.activation(out=warm[:, 1:2], in_=warm[:, 0:1], func=ACTF.Sin)
 
         def xy_row(eng, dst, r, xy, which):
             flat = xy.rearrange("(o c) t -> o (c t)", o=1)
@@ -156,56 +156,48 @@ def tile_claimencoder_w_kernel(
                 ].bitcast(I32),
             )
 
+        def w1_half(g, h):
+            nc.sync.dma_start(
+                out=w1[:, g, 1024 * h:1024 * (h + 1)],
+                in_=W1_words[g].rearrange("p n t -> p (n t)")[
+                    :, 4096 * h:4096 * (h + 1)
+                ].bitcast(I32),
+            )
+
+        sy = nc.sync
+        xy_row(sy, inp_s, 1, src_xy, 0)
+        seg_w(sy, 1, 0, src_wsx)
+        seg_b(sy, 0, src_bsx)
+        seg_w(sy, 1, 1, src_wcx)
+        seg_b(sy, 1, src_bcx)
+        seg_w(sy, 2, 2, src_wsy)
+        xy_row(sy, inp_s, 2, src_xy, 1)
+        w1_half(0, 0)
+        seg_b(sy, 2, src_bsy)
+        seg_w(sy, 2, 3, src_wcy)
+        seg_b(sy, 3, src_bcy)
+        xy_row(sy, inp_d, 3, dst_xy, 0)
+        seg_w(sy, 3, 4, dst_wsx)
+        seg_b(sy, 4, dst_bsx)
+        xy_row(sy, inp_d, 4, dst_xy, 1)
+        w1_half(0, 1)
+        seg_w(sy, 3, 5, dst_wcx)
+        seg_b(sy, 5, dst_bcx)
+        seg_w(sy, 4, 6, dst_wsy)
+        seg_b(sy, 6, dst_bsy)
+        seg_w(sy, 4, 7, dst_wcy)
+        seg_b(sy, 7, dst_bcy)
+        w1_full(1)
+        w1_full(2)
         for q in range(4):
             scale_q(0, W1_scales, 0, q)
-        for g in (0, 1, 2, 5, 6, 7):
-            w1_full(g)
-        for q in range(4):
-            scale_q(1, W1_scales, 4, q)
-        for j in range(4):
-            w1_pair(3, j)
-        for q in range(4):
-            scale_q(2, W2_scales, 0, q)
-        w2_full(0)
-        w2_full(1)
-        w2_pair(0, 512)
-        w2_pair(512, 1024)
-        w2_pair(1024, 1536)
-        w2_pair(1536, 1792)
-        w2_pair(1792, 2048)
-
-        sc = nc.scalar
-        xy_row(sc, inp_s, 1, src_xy, 0)
-        xy_row(sc, inp_s, 2, src_xy, 1)
-        xy_row(sc, inp_d, 3, dst_xy, 0)
-        xy_row(sc, inp_d, 4, dst_xy, 1)
-        seg_w(sc, 1, 0, src_wsx)
-        seg_b(sc, 0, src_bsx)
-        seg_w(sc, 1, 1, src_wcx)
-        seg_b(sc, 1, src_bcx)
-        seg_w(sc, 2, 2, src_wsy)
-        seg_b(sc, 2, src_bsy)
-        seg_w(sc, 2, 3, src_wcy)
-        seg_b(sc, 3, src_bcy)
-        seg_w(sc, 3, 4, dst_wsx)
-        seg_b(sc, 4, dst_bsx)
-        seg_w(sc, 3, 5, dst_wcx)
-        seg_b(sc, 5, dst_bcx)
-        seg_w(sc, 4, 6, dst_wsy)
-        seg_b(sc, 6, dst_bsy)
-        seg_w(sc, 4, 7, dst_wcy)
-        seg_b(sc, 7, dst_bcy)
-        nc.scalar.activation(out=warm[:, 1:2], in_=warm[:, 0:1], func=ACTF.Sin)
 
         nums = ((time_s, t_w, t_b), (wait_src, ws_w, ws_b), (wait_dst, wd_w, wd_b))
         for i, (sv, wv, bv) in enumerate(nums):
             c0 = 2560 + 512 * i
-            gp.dma_start(out=inp_n[5 + i:6 + i, :], in_=row(sv))
+            gp.dma_start(out=inp_n[5 + i:6 + i, i, :], in_=row(sv))
             gp.dma_start(out=par[5 + i:6 + i, c0:c0 + 512], in_=row(wv))
             gp.dma_start(out=par[0:1, c0:c0 + 512], in_=row(bv))
-        gzero(bpar[:])
-        gp.dma_start(out=bpar[0:1, :], in_=row(b1))
-        gp.dma_start(out=bpar[32:33, :], in_=row(b2))
         make_identity(nc, ident[:])
 
         ph_ps = bank(7, [P, 16, 32], F32, "ph_ps")
@@ -219,7 +211,7 @@ def tile_claimencoder_w_kernel(
             out=sbias[:], in0=ph_ps[:, 0:TRIG_G, 0], scalar1=TWO_PI, scalar2=None, op0=ALU.mult
         )
 
-        zbank = {0: 4, 1: 5, 5: 7, 2: 6, 6: 4, 3: 5, 7: 6, 4: 7}
+        zbank = {0: 4, 1: 5, 2: 6, 3: 7, 4: 4, 5: 5, 6: 6, 7: 7}
         zrhs = {0: (inp_s,), 1: (inp_s,), 2: (inp_s, inp_d), 3: (inp_d,), 4: (inp_d,)}
         ztile = {}
         frac_of = {}
@@ -230,7 +222,7 @@ def tile_claimencoder_w_kernel(
             if g < TRIG_G:
                 rhs = [src[:, 0:256:2] for src in zrhs[g]]
             else:
-                rhs = [inp_n[:]]
+                rhs = [inp_n[:, g - TRIG_G, :]]
             for t in range(4):
                 for i, r in enumerate(rhs):
                     nc.tensor.matmul(
@@ -335,66 +327,96 @@ def tile_claimencoder_w_kernel(
         for j in all4:
             acc1[j] = bank(j, [P, NT], F32, "acc1_%d" % j)
         z_block(0)
+        z_block(1)
         trig_v(0)
         trig_s(0)
-        z_block(1)
-        trig_v(1)
-        z_block(5)
-        num(5)
-        quant_f(0)
-        trig_s(1)
+        zero(bpar[:])
+        sy.dma_start(out=bpar[0:1, :], in_=row(b1))
+        sy.dma_start(out=bpar[32:33, :], in_=row(b2))
+        w1_full(3)
+        w1_full(4)
         z_block(2)
-        trig_v(2)
-        z_block(6)
-        num(6)
-        quant_f(1)
-        trig_s(2)
-        l1(0, all4, True, False)
-        quant_f(5)
+        trig_v(1)
+        trig_s(1)
+        quant_f(0)
+        zero(planes[:, 1, :])
+        for q in range(4):
+            scale_q(1, W1_scales, 4, q)
+        w1_full(5)
+        for j in range(4):
+            w1_pair(6, j)
         z_block(3)
+        trig_v(2)
+        trig_s(2)
+        quant_f(1)
+        zero(planes[:, 2, :])
+        for q in range(4):
+            scale_q(2, W2_scales, 0, q)
+        w2_full(0)
+        w2_full(1)
+        w2_pair(0, 512)
+        w2_pair(512, 1024)
+        w2_pair(1024, 1536)
+        w2_pair(1536, 1792)
+        w2_pair(1792, 2048)
+        z_block(4)
         trig_v(3)
         trig_s(3)
-        l1(1, all4, False, False)
         quant_f(2)
+        z_block(5)
+        trig_v(4)
+        trig_s(4)
+        quant_f(3)
+        num(5)
+        quant_f(4)
+        l1(0, all4, True, False)
+        l1(1, all4, False, False)
+        quant_f(5)
+        z_block(6)
+        num(6)
+        l1(2, all4, False, False)
+        for i in range(2):
+            bias_mm(0, i, 4 + i)
+            bias_cp(0, i)
+        l1(3, all4, False, False)
         quant_f(6)
         z_block(7)
         num(7)
-        z_block(4)
-        trig_v(4)
-        trig_s(4)
-        l1(2, all4, False, False)
-        quant_f(3)
+        l1(4, all4, False, False)
+        for i in range(2, 4):
+            bias_mm(0, i, 2 + i)
+            bias_cp(0, i)
         quant_f(7)
         l1(5, all4, False, False)
-        quant_f(4)
-        l1(6, all4, False, False)
-        for i in range(4):
-            bias_mm(0, i, 4 + i % 2)
-            bias_cp(0, i)
-        l1(7, all4, False, False)
-        for j in range(2):
-            l1(3, (j,), False, False)
-            l1(4, (j,), False, True)
+        def l1_last(j):
+            l1(6, (j,), False, False)
+            l1(7, (j,), False, True)
+
+        def bias_out(i):
+            bias_mm(1, i, (6, 7, 6, 1)[i])
+            bias_cp(1, i)
+
+        l1_last(0)
+        l1_last(1)
         h_add(0)
         h_leak(0)
         h_transpose(0)
-        l1(3, (2,), False, False)
-        l1(4, (2,), False, True)
+        bias_out(0)
+        l1_last(2)
         h_add(1)
         h_leak(1)
         quant_h(0)
         h_transpose(1)
-        l1(3, (3,), False, False)
-        l1(4, (3,), False, True)
+        bias_out(1)
+        l1_last(3)
         h_add(2)
         h_leak(2)
         quant_h(1)
         h_transpose(2)
+        bias_out(2)
         h_add(3)
         h_leak(3)
         quant_h(2)
-        h_transpose(3)
-        quant_h(3)
 
         cols = ((0, 512, 4), (512, 1024, 5), (1024, 1536, 6), (1536, 1792, 7), (1792, 2048, 0))
         acc2 = [bank(b, [P, c1 - c0], F32, "acc2_%d" % c0) for c0, c1, b in cols]
@@ -412,9 +434,9 @@ def tile_claimencoder_w_kernel(
 
         for i in range(len(cols)):
             l2(0, i, True, False)
-        for i in range(4):
-            bias_mm(1, i, 1 + i % 2)
-            bias_cp(1, i)
+        h_transpose(3)
+        bias_out(3)
+        quant_h(3)
         for i in range(len(cols)):
             l2(1, i, False, False)
         for i, (c0, c1, b) in enumerate(cols):

@@ -46,6 +46,7 @@ def tile_claimencoder_w_kernel(
         ctx.enter_context(tc.manual_schedule())
         keep = ctx.enter_context(tc.tile_pool(name="keep", bufs=1))
         rot = ctx.enter_context(tc.tile_pool(name="rot", bufs=2))
+        prp = ctx.enter_context(tc.tile_pool(name="prp", bufs=4))
         frp = ctx.enter_context(tc.tile_pool(name="frp", bufs=5))
         outp = ctx.enter_context(tc.tile_pool(name="outp", bufs=4))
         ps = ctx.enter_context(tc.psum_pool(name="ps", bufs=1))
@@ -180,24 +181,29 @@ def tile_claimencoder_w_kernel(
         seg_w(sy, 3, 4, dst_wsx)
         seg_b(sy, 4, dst_bsx)
         xy_row(sy, inp_d, 4, dst_xy, 1)
-        w1_half(0, 1)
+        w1_full(1)
         seg_w(sy, 3, 5, dst_wcx)
         seg_b(sy, 5, dst_bcx)
         seg_w(sy, 4, 6, dst_wsy)
         seg_b(sy, 6, dst_bsy)
         seg_w(sy, 4, 7, dst_wcy)
         seg_b(sy, 7, dst_bcy)
-        w1_full(1)
         w1_full(2)
+        w1_half(0, 1)
         for q in range(4):
             scale_q(0, W1_scales, 0, q)
 
         nums = ((time_s, t_w, t_b), (wait_src, ws_w, ws_b), (wait_dst, wd_w, wd_b))
-        for i, (sv, wv, bv) in enumerate(nums):
+
+        def num_rows(eng, i):
             c0 = 2560 + 512 * i
-            gp.dma_start(out=inp_n[5 + i:6 + i, i, :], in_=row(sv))
-            gp.dma_start(out=par[5 + i:6 + i, c0:c0 + 512], in_=row(wv))
-            gp.dma_start(out=par[0:1, c0:c0 + 512], in_=row(bv))
+            eng.dma_start(out=par[5 + i:6 + i, c0:c0 + 512], in_=row(nums[i][1]))
+            eng.dma_start(out=par[0:1, c0:c0 + 512], in_=row(nums[i][2]))
+
+        for i in range(3):
+            gp.dma_start(out=inp_n[5 + i:6 + i, i, :], in_=row(nums[i][0]))
+            if i < 2:
+                num_rows(gp, i)
         make_identity(nc, ident[:])
 
         ph_ps = bank(7, [P, 16, 32], F32, "ph_ps")
@@ -298,7 +304,7 @@ def tile_claimencoder_w_kernel(
         pre_of = {}
 
         def h_add(j):
-            pre = rot.tile([P, 4, P], F32, tag="pre", name="pre")
+            pre = prp.tile([P, 4, P], F32, tag="pre", name="pre")
             pre_of[j] = pre
             nc.vector.tensor_tensor(
                 out=pre[:], in0=acc1[j][:].rearrange("p (c t) -> p t c", t=4),
@@ -330,11 +336,12 @@ def tile_claimencoder_w_kernel(
         z_block(1)
         trig_v(0)
         trig_s(0)
+        num_rows(sy, 2)
+        w1_full(3)
+        w1_full(4)
         zero(bpar[:])
         sy.dma_start(out=bpar[0:1, :], in_=row(b1))
         sy.dma_start(out=bpar[32:33, :], in_=row(b2))
-        w1_full(3)
-        w1_full(4)
         z_block(2)
         trig_v(1)
         trig_s(1)
@@ -375,48 +382,46 @@ def tile_claimencoder_w_kernel(
         z_block(6)
         num(6)
         l1(2, all4, False, False)
-        for i in range(2):
+        z_block(7)
+        quant_f(6)
+        num(7)
+        l1(3, all4, False, False)
+        quant_f(7)
+        l1(4, all4, False, False)
+        for i in range(4):
             bias_mm(0, i, 4 + i)
             bias_cp(0, i)
-        l1(3, all4, False, False)
-        quant_f(6)
-        z_block(7)
-        num(7)
-        l1(4, all4, False, False)
-        for i in range(2, 4):
-            bias_mm(0, i, 2 + i)
-            bias_cp(0, i)
-        quant_f(7)
         l1(5, all4, False, False)
         def l1_last(j):
             l1(6, (j,), False, False)
             l1(7, (j,), False, True)
 
         def bias_out(i):
-            bias_mm(1, i, (6, 7, 6, 1)[i])
+            bias_mm(1, i, 4 + i)
             bias_cp(1, i)
 
-        l1_last(0)
-        l1_last(1)
+        for j in range(4):
+            l1_last(j)
         h_add(0)
+        h_add(1)
         h_leak(0)
         h_transpose(0)
         bias_out(0)
-        l1_last(2)
-        h_add(1)
         h_leak(1)
-        quant_h(0)
         h_transpose(1)
         bias_out(1)
-        l1_last(3)
         h_add(2)
+        h_add(3)
         h_leak(2)
-        quant_h(1)
         h_transpose(2)
         bias_out(2)
-        h_add(3)
+        quant_h(0)
         h_leak(3)
+        h_transpose(3)
+        bias_out(3)
+        quant_h(1)
         quant_h(2)
+        quant_h(3)
 
         cols = ((0, 512, 4), (512, 1024, 5), (1024, 1536, 6), (1536, 1792, 7), (1792, 2048, 0))
         acc2 = [bank(b, [P, c1 - c0], F32, "acc2_%d" % c0) for c0, c1, b in cols]
@@ -434,9 +439,6 @@ def tile_claimencoder_w_kernel(
 
         for i in range(len(cols)):
             l2(0, i, True, False)
-        h_transpose(3)
-        bias_out(3)
-        quant_h(3)
         for i in range(len(cols)):
             l2(1, i, False, False)
         for i, (c0, c1, b) in enumerate(cols):

@@ -48,7 +48,7 @@ def tile_claimencoder_w_kernel(
         rot = ctx.enter_context(tc.tile_pool(name="rot", bufs=2))
         prp = ctx.enter_context(tc.tile_pool(name="prp", bufs=4))
         frp = ctx.enter_context(tc.tile_pool(name="frp", bufs=5))
-        outp = ctx.enter_context(tc.tile_pool(name="outp", bufs=4))
+        outp = ctx.enter_context(tc.tile_pool(name="outp", bufs=5))
         ps = ctx.enter_context(tc.psum_pool(name="ps", bufs=1))
 
         def bank(i, shape, dtype, name):
@@ -133,14 +133,6 @@ def tile_claimencoder_w_kernel(
                 out=w1[:, g, :], in_=W1_words[g].rearrange("p n t -> p (n t)").bitcast(I32)
             )
 
-        def w1_pair(g, j):
-            nc.sync.dma_start(
-                out=w1[:, g:g + 2, NT * j:NT * (j + 1)],
-                in_=W1_words[g:g + 2].rearrange("g p n t -> p g (n t)")[
-                    :, :, 4 * NT * j:4 * NT * (j + 1)
-                ].bitcast(I32),
-            )
-
         gp = nc.gpsimd
 
         def w2_full(g):
@@ -149,12 +141,10 @@ def tile_claimencoder_w_kernel(
                 in_=W2_words[g].rearrange("p n t -> p (n t)").bitcast(I32),
             )
 
-        def w2_pair(c0, c1):
+        def w2_part(g, c0, c1):
             nc.sync.dma_start(
-                out=w2[:, 2:4, c0:c1],
-                in_=W2_words[2:4].rearrange("g p n t -> p g (n t)")[
-                    :, :, 4 * c0:4 * c1
-                ].bitcast(I32),
+                out=w2[:, g, c0:c1],
+                in_=W2_words[g].rearrange("p n t -> p (n t)")[:, 4 * c0:4 * c1].bitcast(I32),
             )
 
         def w1_half(g, h):
@@ -166,6 +156,7 @@ def tile_claimencoder_w_kernel(
             )
 
         sy = nc.sync
+        w1_half(0, 0)
         xy_row(sy, inp_s, 1, src_xy, 0)
         seg_w(sy, 1, 0, src_wsx)
         seg_b(sy, 0, src_bsx)
@@ -173,7 +164,6 @@ def tile_claimencoder_w_kernel(
         seg_b(sy, 1, src_bcx)
         seg_w(sy, 2, 2, src_wsy)
         xy_row(sy, inp_s, 2, src_xy, 1)
-        w1_half(0, 0)
         seg_b(sy, 2, src_bsy)
         seg_w(sy, 2, 3, src_wcy)
         seg_b(sy, 3, src_bcy)
@@ -350,8 +340,9 @@ def tile_claimencoder_w_kernel(
         for q in range(4):
             scale_q(1, W1_scales, 4, q)
         w1_full(5)
-        for j in range(4):
-            w1_pair(6, j)
+        w1_full(6)
+        w1_half(7, 0)
+        w1_half(7, 1)
         z_block(3)
         trig_v(2)
         trig_s(2)
@@ -361,11 +352,11 @@ def tile_claimencoder_w_kernel(
             scale_q(2, W2_scales, 0, q)
         w2_full(0)
         w2_full(1)
-        w2_pair(0, 512)
-        w2_pair(512, 1024)
-        w2_pair(1024, 1536)
-        w2_pair(1536, 1792)
-        w2_pair(1792, 2048)
+        w2_part(2, 0, 1024)
+        w2_part(3, 0, 1024)
+        w2_part(2, 1024, 2048)
+        w2_part(3, 1024, 1536)
+        w2_part(3, 1536, 2048)
         z_block(4)
         trig_v(3)
         trig_s(3)
@@ -376,12 +367,12 @@ def tile_claimencoder_w_kernel(
         quant_f(3)
         num(5)
         quant_f(4)
-        l1(0, all4, True, False)
-        l1(1, all4, False, False)
+        l1(1, all4, True, False)
+        l1(2, all4, False, False)
         quant_f(5)
         z_block(6)
         num(6)
-        l1(2, all4, False, False)
+        l1(0, all4, False, False)
         z_block(7)
         quant_f(6)
         num(7)
@@ -392,36 +383,34 @@ def tile_claimencoder_w_kernel(
             bias_mm(0, i, 4 + i)
             bias_cp(0, i)
         l1(5, all4, False, False)
+        l1(6, all4, False, False)
         def l1_last(j):
-            l1(6, (j,), False, False)
             l1(7, (j,), False, True)
 
         def bias_out(i):
             bias_mm(1, i, 4 + i)
             bias_cp(1, i)
 
-        for j in range(4):
-            l1_last(j)
+        l1_last(0)
+        l1_last(1)
+        for i in range(4):
+            bias_out(i)
         h_add(0)
+        l1_last(2)
         h_add(1)
         h_leak(0)
         h_transpose(0)
-        bias_out(0)
+        l1_last(3)
         h_leak(1)
         h_transpose(1)
-        bias_out(1)
         h_add(2)
         h_add(3)
         h_leak(2)
         h_transpose(2)
-        bias_out(2)
         quant_h(0)
         h_leak(3)
-        h_transpose(3)
-        bias_out(3)
         quant_h(1)
         quant_h(2)
-        quant_h(3)
 
         cols = ((0, 512, 4), (512, 1024, 5), (1024, 1536, 6), (1536, 1792, 7), (1792, 2048, 0))
         acc2 = [bank(b, [P, c1 - c0], F32, "acc2_%d" % c0) for c0, c1, b in cols]
@@ -439,12 +428,14 @@ def tile_claimencoder_w_kernel(
 
         for i in range(len(cols)):
             l2(0, i, True, False)
+        h_transpose(3)
+        quant_h(3)
         for i in range(len(cols)):
             l2(1, i, False, False)
         for i, (c0, c1, b) in enumerate(cols):
             l2(2, i, False, False)
             l2(3, i, False, True)
-            pre = rot.tile([P, NT], F32, tag="preo", name="preo")
+            pre = outp.tile([P, NT], F32, tag="preo", name="preo")
             res = outp.tile([P, NT], F32, tag="res", name="res")
             n = c1 - c0
             nc.vector.tensor_tensor(

@@ -157,27 +157,28 @@ def tile_claimencoder_w_kernel(
 
         sy = nc.sync
         w1_half(0, 0)
+        sc = nc.scalar
         xy_row(sy, inp_s, 1, src_xy, 0)
+        seg_b(sc, 0, src_bsx)
         seg_w(sy, 1, 0, src_wsx)
-        seg_b(sy, 0, src_bsx)
+        seg_b(sc, 1, src_bcx)
         seg_w(sy, 1, 1, src_wcx)
-        seg_b(sy, 1, src_bcx)
+        xy_row(sc, inp_s, 2, src_xy, 1)
         seg_w(sy, 2, 2, src_wsy)
-        xy_row(sy, inp_s, 2, src_xy, 1)
+        seg_w(sc, 2, 3, src_wcy)
         seg_b(sy, 2, src_bsy)
-        seg_w(sy, 2, 3, src_wcy)
-        seg_b(sy, 3, src_bcy)
-        xy_row(sy, inp_d, 3, dst_xy, 0)
+        seg_b(sc, 3, src_bcy)
         seg_w(sy, 3, 4, dst_wsx)
+        xy_row(sc, inp_d, 3, dst_xy, 0)
         seg_b(sy, 4, dst_bsx)
-        xy_row(sy, inp_d, 4, dst_xy, 1)
+        xy_row(sc, inp_d, 4, dst_xy, 1)
         w1_full(1)
         seg_w(sy, 3, 5, dst_wcx)
-        seg_b(sy, 5, dst_bcx)
+        seg_b(sc, 5, dst_bcx)
         seg_w(sy, 4, 6, dst_wsy)
-        seg_b(sy, 6, dst_bsy)
+        seg_b(sc, 6, dst_bsy)
         seg_w(sy, 4, 7, dst_wcy)
-        seg_b(sy, 7, dst_bcy)
+        seg_b(sc, 7, dst_bcy)
         w1_full(2)
         w1_half(0, 1)
         for q in range(4):

@@ -102,10 +102,6 @@ def tile_claimencoder_w_kernel(
             nc.gpsimd.memset(ap.bitcast(I32), 0)
 
         nc.gpsimd.memset(warm[:], 0.0)
-        gzero(par[:, 1920:2560])
-        gzero(inp_n[:].rearrange("p i c -> p (i c)"))
-        nc.gpsimd.memset(inp_n[0:1, :, :], 1.0)
-        gzero(par[:, 2560:4096])
         nc.scalar.activation(out=warm[:, 1:2], in_=warm[:, 0:1], func=ACTF.Sin)
 
         def xy_row(eng, dst, r, xy, which):
@@ -173,16 +169,10 @@ def tile_claimencoder_w_kernel(
         seg_b(sy, 4, dst_bsx)
         xy_row(sc, inp_d, 4, dst_xy, 1)
         w1_full(1)
-        seg_w(sy, 3, 5, dst_wcx)
-        seg_b(sc, 5, dst_bcx)
-        seg_w(sy, 4, 6, dst_wsy)
-        seg_b(sc, 6, dst_bsy)
-        seg_w(sy, 4, 7, dst_wcy)
-        seg_b(sc, 7, dst_bcy)
-        w1_full(2)
-        w1_half(0, 1)
         for q in range(4):
             scale_q(0, W1_scales, 0, q)
+        w1_full(2)
+        w1_half(0, 1)
 
         nums = ((time_s, t_w, t_b), (wait_src, ws_w, ws_b), (wait_dst, wd_w, wd_b))
 
@@ -191,10 +181,19 @@ def tile_claimencoder_w_kernel(
             eng.dma_start(out=par[5 + i:6 + i, c0:c0 + 512], in_=row(nums[i][1]))
             eng.dma_start(out=par[0:1, c0:c0 + 512], in_=row(nums[i][2]))
 
+        gzero(par[:, 1920:2560])
+        seg_w(gp, 4, 6, dst_wsy)
+        seg_b(gp, 6, dst_bsy)
+        seg_w(gp, 4, 7, dst_wcy)
+        seg_b(gp, 7, dst_bcy)
+        seg_w(gp, 3, 5, dst_wcx)
+        seg_b(gp, 5, dst_bcx)
+        gzero(inp_n[:].rearrange("p i c -> p (i c)"))
+        nc.gpsimd.memset(inp_n[0:1, :, :], 1.0)
+        gzero(par[:, 2560:4096])
         for i in range(3):
             gp.dma_start(out=inp_n[5 + i:6 + i, i, :], in_=row(nums[i][0]))
-            if i < 2:
-                num_rows(gp, i)
+            num_rows(gp, i)
         make_identity(nc, ident[:])
 
         ph_ps = bank(7, [P, 16, 32], F32, "ph_ps")
@@ -327,7 +326,6 @@ def tile_claimencoder_w_kernel(
         z_block(1)
         trig_v(0)
         trig_s(0)
-        num_rows(sy, 2)
         w1_full(3)
         w1_full(4)
         zero(bpar[:])
@@ -362,29 +360,30 @@ def tile_claimencoder_w_kernel(
         trig_v(3)
         trig_s(3)
         quant_f(2)
-        z_block(5)
+        l1(1, all4, True, False)
         trig_v(4)
         trig_s(4)
         quant_f(3)
+        l1(2, all4, False, False)
+        z_block(5)
         num(5)
         quant_f(4)
-        l1(1, all4, True, False)
-        l1(2, all4, False, False)
-        quant_f(5)
+        l1(0, all4, False, False)
         z_block(6)
         num(6)
-        l1(0, all4, False, False)
-        z_block(7)
-        quant_f(6)
-        num(7)
+        quant_f(5)
         l1(3, all4, False, False)
-        quant_f(7)
+        z_block(7)
+        num(7)
+        quant_f(6)
         l1(4, all4, False, False)
+        quant_f(7)
         for i in range(4):
             bias_mm(0, i, 4 + i)
             bias_cp(0, i)
         l1(5, all4, False, False)
         l1(6, all4, False, False)
+
         def l1_last(j):
             l1(7, (j,), False, True)
 
@@ -433,17 +432,31 @@ def tile_claimencoder_w_kernel(
         quant_h(3)
         for i in range(len(cols)):
             l2(1, i, False, False)
-        for i, (c0, c1, b) in enumerate(cols):
+        pre_out = {}
+
+        def out_add(i):
+            c0, c1, b = cols[i]
+            pre = outp.tile([P, NT], F32, tag="preo", name="preo")
+            pre_out[i] = pre
+            nc.vector.tensor_tensor(
+                out=pre[:, 0:c1 - c0], in0=acc2[i][:], in1=bbo[:, c0:c1], op=ALU.add
+            )
+
+        def out_leak(i):
+            c0, c1, b = cols[i]
+            pre = pre_out[i]
+            res = outp.tile([P, NT], F32, tag="res", name="res")
+            nc.vector.scalar_tensor_tensor(
+                out=res[:, 0:c1 - c0], in0=pre[:, 0:c1 - c0], scalar=0.01,
+                in1=pre[:, 0:c1 - c0], op0=ALU.mult, op1=ALU.max,
+            )
+            nc.sync.dma_start(out=out[:, c0:c1], in_=res[:, 0:c1 - c0])
+
+        for i in range(len(cols)):
             l2(2, i, False, False)
             l2(3, i, False, True)
-            pre = outp.tile([P, NT], F32, tag="preo", name="preo")
-            res = outp.tile([P, NT], F32, tag="res", name="res")
-            n = c1 - c0
-            nc.vector.tensor_tensor(
-                out=pre[:, 0:n], in0=acc2[i][:], in1=bbo[:, c0:c1], op=ALU.add
-            )
-            nc.vector.scalar_tensor_tensor(
-                out=res[:, 0:n], in0=pre[:, 0:n], scalar=0.01, in1=pre[:, 0:n],
-                op0=ALU.mult, op1=ALU.max,
-            )
-            nc.sync.dma_start(out=out[:, c0:c1], in_=res[:, 0:n])
+        for group in ((0, 1), (2,), (3, 4)):
+            for i in group:
+                out_add(i)
+            for i in group:
+                out_leak(i)

import math
from contextlib import ExitStack

import concourse.bass as bass
import concourse.mybir as mybir
import concourse.tile as tile
from concourse.masks import make_identity

F32 = mybir.dt.float32
BF16 = mybir.dt.bfloat16
I32 = mybir.dt.int32
U32 = mybir.dt.uint32
U8 = mybir.dt.uint8
FP8X4 = mybir.dt.float8_e4m3fn_x4
ALU = mybir.AluOpType
ACTF = mybir.ActivationFunctionType

P = 128
FEAT = 4096
HID = 2048
G1 = 8
G2 = 4
NT = 512
TRIG_G = 5
SEG = 320
FLOPS = 2 * 128 * (FEAT * HID + HID * HID)
TWO_PI = 2.0 * math.pi
INV_TWO_PI = 1.0 / TWO_PI


def row(vec):
    return vec.rearrange("(o n) -> o n", o=1)


def tile_claimencoder_w_kernel(
    tc,
    src_xy, dst_xy, time_s, wait_src, wait_dst,
    src_wsx, src_bsx, src_wcx, src_bcx, src_wsy, src_bsy, src_wcy, src_bcy,
    dst_wsx, dst_bsx, dst_wcx, dst_bcx, dst_wsy, dst_bsy, dst_wcy, dst_bcy,
    t_w, t_b, ws_w, ws_b, wd_w, wd_b,
    W1_words, W1_scales, b1, W2_words, W2_scales, b2,
    out,
):
    nc = tc.nc
    with ExitStack() as ctx:
        ctx.enter_context(tc.manual_schedule())
        keep = ctx.enter_context(tc.tile_pool(name="keep", bufs=1))
        rot = ctx.enter_context(tc.tile_pool(name="rot", bufs=2))
        prp = ctx.enter_context(tc.tile_pool(name="prp", bufs=4))
        frp = ctx.enter_context(tc.tile_pool(name="frp", bufs=5))
        outp = ctx.enter_context(tc.tile_pool(name="outp", bufs=5))
        ps = ctx.enter_context(tc.psum_pool(name="ps", bufs=1))

        def bank(i, shape, dtype, name):
            return ps.tile(shape, dtype, tag="b%d" % i, name=name)

        par = keep.tile([P, FEAT], BF16, name="par")
        inp_s = keep.tile([P, 256], BF16, name="inp_s")
        inp_d = keep.tile([P, 256], BF16, name="inp_d")
        inp_n = keep.tile([P, 3, P], BF16, name="inp_n")
        cst = keep.tile([P, 288], BF16, name="cst")
        bpar = keep.tile([P, HID], BF16, name="bpar")
        cosi = keep.tile([P, 640], BF16, name="cosi")
        warm = keep.tile([P, 2], F32, name="warm")
        ident = keep.tile([P, P], BF16, name="ident")
        planes = keep.tile([P, 3, HID], U8, name="planes", align_bytes=64)
        w1 = keep.tile([P, G1, HID], I32, name="w1", align_bytes=64)
        w2 = keep.tile([P, G2, HID], I32, name="w2", align_bytes=64)
        phase = keep.tile([P, TRIG_G], F32, name="phase")
        sbias = keep.tile([P, TRIG_G], F32, name="sbias")
        fgrp = keep.tile([P, G1, P, 4], BF16, name="fgrp", align_bytes=64)
        fcod = keep.tile([P, G1, P], U32, name="fcod", align_bytes=64)
        fscl = keep.tile([P, G1, P], U8, name="fscl", align_bytes=64)
        bbh = keep.tile([P, G2, 4, P], BF16, name="bbh")
        bbo = keep.tile([P, HID], BF16, name="bbo")
        hb = keep.tile([P, G2, 4, P], BF16, name="hb")
        hgrp = keep.tile([P, G2, P, 4], BF16, name="hgrp", align_bytes=64)
        hcod = keep.tile([P, G2, P], U32, name="hcod", align_bytes=64)
        hscl = keep.tile([P, G2, P], U8, name="hscl", align_bytes=64)

        def zero(ap):
            nc.vector.memset(ap.bitcast(I32), 0)

        zero(inp_s[:])
        nc.vector.memset(inp_s[0:1, :], 1.0)
        zero(par[:, 0:640])
        zero(par[:, 640:1280])
        zero(inp_d[:])
        nc.vector.memset(inp_d[32:33, :], 1.0)
        zero(par[:, 1280:1920])
        zero(cst[:])
        nc.vector.memset(cst[0:1, 0:32], 0.25)
        zero(cosi[:])
        nc.vector.memset(
            cosi[0:1, :].rearrange("o (s h c) -> o s h c", h=2, c=80)[:, :, 1, :], 1.0
        )
        zero(planes[:, 0, :])
        nc.vector.memset(cst[0:1, 32:160], 1.0)
        nc.vector.memset(cst[32:33, 160:288], 1.0)

        def gzero(ap):
            nc.gpsimd.memset(ap.bitcast(I32), 0)

        nc.gpsimd.memset(warm[:], 0.0)
        nc.scalar.activation(out=warm[:, 1:2], in_=warm[:, 0:1], func=ACTF.Sin)

        def xy_row(eng, dst, r, xy, which):
            flat = xy.rearrange("(o c) t -> o (c t)", o=1)
            if which == 0:
                eng.dma_start(out=dst[r:r + 1, 0:256], in_=flat)
            else:
                eng.dma_start(out=dst[r:r + 1, 0:255], in_=flat[:, 1:256])

        def seg_w(eng, r, s, wv):
            eng.dma_start(out=par[r:r + 1, SEG * s:SEG * (s + 1)], in_=row(wv))

        def seg_b(eng, s, bv):
            r = 0 if s < 4 else 32
            eng.dma_start(out=par[r:r + 1, SEG * s:SEG * (s + 1)], in_=row(bv))

        def scale_q(a, scales, g0, q):
            nc.sync.dma_start(
                out=planes[32 * q:32 * q + 16, a, :].bitcast(I32),
                in_=scales[g0:g0 + 4, 4 * q:4 * q + 4, :].bitcast(I32),
            )

        def w1_full(g):
            nc.sync.dma_start(
                out=w1[:, g, :], in_=W1_words[g].rearrange("p n t -> p (n t)").bitcast(I32)
            )

        gp = nc.gpsimd

        def w2_full(g):
            nc.sync.dma_start(
                out=w2[:, g, :],
                in_=W2_words[g].rearrange("p n t -> p (n t)").bitcast(I32),
            )

        def w2_part(g, c0, c1):
            nc.sync.dma_start(
                out=w2[:, g, c0:c1],
                in_=W2_words[g].rearrange("p n t -> p (n t)")[:, 4 * c0:4 * c1].bitcast(I32),
            )

        def w1_half(g, h):
            nc.sync.dma_start(
                out=w1[:, g, 1024 * h:1024 * (h + 1)],
                in_=W1_words[g].rearrange("p n t -> p (n t)")[
                    :, 4096 * h:4096 * (h + 1)
                ].bitcast(I32),
            )

        sy = nc.sync
        w1_half(0, 0)
        sc = nc.scalar
        xy_row(sy, inp_s, 1, src_xy, 0)
        seg_b(sc, 0, src_bsx)
        seg_w(sy, 1, 0, src_wsx)
        seg_b(sc, 1, src_bcx)
        seg_w(sy, 1, 1, src_wcx)
        xy_row(sc, inp_s, 2, src_xy, 1)
        seg_w(sy, 2, 2, src_wsy)
        seg_w(sc, 2, 3, src_wcy)
        seg_b(sy, 2, src_bsy)
        seg_b(sc, 3, src_bcy)
        seg_w(sy, 3, 4, dst_wsx)
        xy_row(sc, inp_d, 3, dst_xy, 0)
        seg_b(sy, 4, dst_bsx)
        xy_row(sc, inp_d, 4, dst_xy, 1)
        w1_full(1)
        for q in range(4):
            scale_q(0, W1_scales, 0, q)
        w1_full(2)
        w1_half(0, 1)

        nums = ((time_s, t_w, t_b), (wait_src, ws_w, ws_b), (wait_dst, wd_w, wd_b))

        def num_rows(eng, i):
            c0 = 2560 + 512 * i
            eng.dma_start(out=par[5 + i:6 + i, c0:c0 + 512], in_=row(nums[i][1]))
            eng.dma_start(out=par[0:1, c0:c0 + 512], in_=row(nums[i][2]))

        gzero(par[:, 1920:2560])
        seg_w(gp, 4, 6, dst_wsy)
        seg_b(gp, 6, dst_bsy)
        seg_w(gp, 4, 7, dst_wcy)
        seg_b(gp, 7, dst_bcy)
        seg_w(gp, 3, 5, dst_wcx)
        seg_b(gp, 5, dst_bcx)
        gzero(inp_n[:].rearrange("p i c -> p (i c)"))
        nc.gpsimd.memset(inp_n[0:1, :, :], 1.0)
        gzero(par[:, 2560:4096])
        for i in range(3):
            gp.dma_start(out=inp_n[5 + i:6 + i, i, :], in_=row(nums[i][0]))
            num_rows(gp, i)
        make_identity(nc, ident[:])

        ph_ps = bank(7, [P, 16, 32], F32, "ph_ps")
        for g in range(TRIG_G):
            nc.tensor.matmul(
                out=ph_ps[:, g, :], lhsT=cosi[:, P * g:P * (g + 1)], rhs=cst[:, 0:32],
                start=True, stop=True,
            )
        nc.vector.tensor_copy(out=phase[:], in_=ph_ps[:, 0:TRIG_G, 0])
        nc.vector.tensor_scalar(
            out=sbias[:], in0=ph_ps[:, 0:TRIG_G, 0], scalar1=TWO_PI, scalar2=None, op0=ALU.mult
        )

        zbank = {0: 4, 1: 5, 2: 6, 3: 7, 4: 4, 5: 5, 6: 6, 7: 7}
        zrhs = {0: (inp_s,), 1: (inp_s,), 2: (inp_s, inp_d), 3: (inp_d,), 4: (inp_d,)}
        ztile = {}
        frac_of = {}

        def z_block(g):
            zb = bank(zbank[g], [P, 4, P], F32, "z%d" % g)
            ztile[g] = zb
            if g < TRIG_G:
                rhs = [src[:, 0:256:2] for src in zrhs[g]]
            else:
                rhs = [inp_n[:, g - TRIG_G, :]]
            for t in range(4):
                for i, r in enumerate(rhs):
                    nc.tensor.matmul(
                        out=zb[:, t, :], lhsT=par[:, 512 * g + t:512 * (g + 1):4], rhs=r,
                        start=(i == 0), stop=(i == len(rhs) - 1),
                    )

        def trig_v(g):
            zf = ztile[g][:].rearrange("p t c -> p (t c)")
            turns = rot.tile([P, NT], I32, tag="turns", name="turns")
            frac = frp.tile([P, NT], F32, tag="frac", name="frac")
            frac_of[g] = frac
            nc.vector.tensor_scalar(
                out=turns[:], in0=zf, scalar1=INV_TWO_PI, scalar2=phase[:, g:g + 1],
                op0=ALU.mult, op1=ALU.add,
            )
            nc.vector.scalar_tensor_tensor(
                out=frac[:], in0=zf, scalar=INV_TWO_PI, in1=turns[:],
                op0=ALU.mult, op1=ALU.subtract,
            )

        def trig_s(g):
            nc.scalar.activation(
                out=fgrp[:, g], in_=frac_of[g][:].rearrange("p (t c) -> p c t", t=4),
                func=ACTF.Sin, bias=sbias[:, g:g + 1], scale=TWO_PI,
            )

        def num(g):
            zb = ztile[g]
            leak = rot.tile([P, 4, P], F32, tag="leak", name="leak")
            nc.scalar.activation(out=leak[:], in_=zb[:], func=ACTF.Copy, scale=0.01)
            nc.vector.tensor_tensor(
                out=fgrp[:, g], in0=zb[:].rearrange("p t c -> p c t"),
                in1=leak[:].rearrange("p t c -> p c t"), op=ALU.max,
            )

        def quant_f(g):
            nc.vector.quantize_mx(
                out=fcod[:, g, :].bitcast(FP8X4), scales=fscl[:, g, :],
                in_=fgrp[:, g].rearrange("p c t -> p (c t)"),
            )

        acc1 = {}

        def l1(g, tiles, first, last):
            k = 4 * (g % 4)
            for j in tiles:
                nc.tensor.matmul_mx(
                    out=acc1[j][:],
                    lhsT=fcod[:, g, :].bitcast(FP8X4), lhsT_scale=fscl[:, g, :],
                    rhs=w1[:, g, NT * j:NT * (j + 1)].bitcast(FP8X4),
                    rhs_scale=planes[k:P, g // 4, NT * j:NT * (j + 1)],
                    start=first, stop=last,
                )

        bb_of = {}

        def bias_mm(layer, i, b):
            bb = bank(b, [P, NT], F32, "bb%d_%d" % (layer, i))
            bb_of[(layer, i)] = bb
            nc.tensor.matmul(
                out=bb[:], lhsT=cst[:, 32 + P * layer:32 + P * (layer + 1)],
                rhs=bpar[:, NT * i:NT * (i + 1)], start=True, stop=True,
            )

        def bias_cp(layer, i):
            bb = bb_of[(layer, i)]
            if layer == 0:
                nc.scalar.copy(out=bbh[:, i], in_=bb[:].rearrange("p (c t) -> p t c", t=4))
            else:
                nc.scalar.copy(out=bbo[:, NT * i:NT * (i + 1)], in_=bb[:])

        pre_of = {}

        def h_add(j):
            pre = prp.tile([P, 4, P], F32, tag="pre", name="pre")
            pre_of[j] = pre
            nc.vector.tensor_tensor(
                out=pre[:], in0=acc1[j][:].rearrange("p (c t) -> p t c", t=4),
                in1=bbh[:, j], op=ALU.add,
            )

        def h_leak(j):
            pre = pre_of[j][:]
            nc.vector.scalar_tensor_tensor(
                out=hb[:, j], in0=pre, scalar=0.01, in1=pre, op0=ALU.mult, op1=ALU.max
            )

        def h_transpose(j):
            xt = bank(j, [P, 8, P], BF16, "xt%d" % j)
            for t in range(4):
                nc.tensor.transpose(out=xt[:, t, :], in_=hb[:, j, t, :], identity=ident[:])
            nc.scalar.copy(out=hgrp[:, j], in_=xt[:, 0:4, :].rearrange("p t c -> p c t"))

        def quant_h(j):
            nc.vector.quantize_mx(
                out=hcod[:, j, :].bitcast(FP8X4), scales=hscl[:, j, :],
                in_=hgrp[:, j].rearrange("p c t -> p (c t)"),
            )

        all4 = (0, 1, 2, 3)
        for j in all4:
            acc1[j] = bank(j, [P, NT], F32, "acc1_%d" % j)
        z_block(0)
        z_block(1)
        trig_v(0)
        trig_s(0)
        w1_full(3)
        w1_full(4)
        zero(bpar[:])
        sy.dma_start(out=bpar[0:1, :], in_=row(b1))
        sy.dma_start(out=bpar[32:33, :], in_=row(b2))
        z_block(2)
        trig_v(1)
        trig_s(1)
        quant_f(0)
        zero(planes[:, 1, :])
        for q in range(4):
            scale_q(1, W1_scales, 4, q)
        w1_full(5)
        w1_full(6)
        w1_half(7, 0)
        w1_half(7, 1)
        z_block(3)
        trig_v(2)
        trig_s(2)
        quant_f(1)
        zero(planes[:, 2, :])
        for q in range(4):
            scale_q(2, W2_scales, 0, q)
        w2_full(0)
        w2_full(1)
        w2_part(2, 0, 1024)
        w2_part(3, 0, 1024)
        w2_part(2, 1024, 2048)
        w2_part(3, 1024, 1536)
        w2_part(3, 1536, 2048)
        z_block(4)
        trig_v(3)
        trig_s(3)
        quant_f(2)
        l1(1, all4, True, False)
        trig_v(4)
        trig_s(4)
        quant_f(3)
        l1(2, all4, False, False)
        z_block(5)
        num(5)
        quant_f(4)
        l1(0, all4, False, False)
        z_block(6)
        num(6)
        quant_f(5)
        l1(3, all4, False, False)
        z_block(7)
        num(7)
        quant_f(6)
        l1(4, all4, False, False)
        quant_f(7)
        for i in range(4):
            bias_mm(0, i, 4 + i)
            bias_cp(0, i)
        l1(5, all4, False, False)
        l1(6, all4, False, False)

        def l1_last(j):
            l1(7, (j,), False, True)

        def bias_out(i):
            bias_mm(1, i, 4 + i)
            bias_cp(1, i)

        l1_last(0)
        l1_last(1)
        for i in range(4):
            bias_out(i)
        h_add(0)
        l1_last(2)
        h_add(1)
        h_leak(0)
        h_transpose(0)
        l1_last(3)
        h_leak(1)
        h_transpose(1)
        h_add(2)
        h_add(3)
        h_leak(2)
        h_transpose(2)
        quant_h(0)
        h_leak(3)
        quant_h(1)
        quant_h(2)

        cols = ((0, 512, 4), (512, 1024, 5), (1024, 1536, 6), (1536, 1792, 7), (1792, 2048, 0))
        acc2 = [bank(b, [P, c1 - c0], F32, "acc2_%d" % c0) for c0, c1, b in cols]

        def l2(g, i, first, last):
            k = 4 * g
            c0, c1, b = cols[i]
            nc.tensor.matmul_mx(
                out=acc2[i][:],
                lhsT=hcod[:, g, :].bitcast(FP8X4), lhsT_scale=hscl[:, g, :],
                rhs=w2[:, g, c0:c1].bitcast(FP8X4),
                rhs_scale=planes[k:P, 2, c0:c1],
                start=first, stop=last,
            )

        for i in range(len(cols)):
            l2(0, i, True, False)
        h_transpose(3)
        quant_h(3)
        for i in range(len(cols)):
            l2(1, i, False, False)
        pre_out = {}

        def out_add(i):
            c0, c1, b = cols[i]
            pre = outp.tile([P, NT], F32, tag="preo", name="preo")
            pre_out[i] = pre
            nc.vector.tensor_tensor(
                out=pre[:, 0:c1 - c0], in0=acc2[i][:], in1=bbo[:, c0:c1], op=ALU.add
            )

        def out_leak(i):
            c0, c1, b = cols[i]
            pre = pre_out[i]
            res = outp.tile([P, NT], F32, tag="res", name="res")
            nc.vector.scalar_tensor_tensor(
                out=res[:, 0:c1 - c0], in0=pre[:, 0:c1 - c0], scalar=0.01,
                in1=pre[:, 0:c1 - c0], op0=ALU.mult, op1=ALU.max,
            )
            nc.sync.dma_start(out=out[:, c0:c1], in_=res[:, 0:c1 - c0])

        for i in range(len(cols)):
            l2(2, i, False, False)
            l2(3, i, False, True)
        for group in ((0, 1), (2,), (3, 4)):
            for i in group:
                out_add(i)
            for i in group:
                out_leak(i)
